import numpy as np
import ml_dtypes


def mxq(x, axis, fmt="e4m3"):
    dtype, down = {"e4m3": (ml_dtypes.float8_e4m3fn, 7), "e5m2": (ml_dtypes.float8_e5m2, 14)}[fmt]
    v = np.moveaxis(np.asarray(x, np.float32).astype(ml_dtypes.bfloat16).astype(np.float64), axis, -1)
    blocks = v.reshape(v.shape[:-1] + (-1, 32))
    amax = np.abs(blocks).max(-1, keepdims=True)
    byte = np.maximum(np.where(amax > 0, np.frexp(amax)[1] - 1 + 127, 0) - down, 1)
    scale = np.exp2(byte - 127.0)
    codes = (blocks / scale).astype(np.float32).astype(dtype).astype(np.float64)
    return np.moveaxis((codes * scale).reshape(v.shape), -1, axis)


WIDE = False


def mx_kscale(k):
    if not WIDE:
        return np.ones(k)
    levels = np.array([10, -10, 5, -5, 0])
    a = np.random.permutation(np.resize(levels, k // 512 * 4)).reshape(k // 512, 4)
    idx = np.arange(k)
    return np.exp2(a[idx // 512, idx % 128 // 32])


BF16 = ml_dtypes.bfloat16


def bf(x):
    return np.asarray(x, np.float32).astype(BF16)


def f64(x):
    return np.asarray(x).astype(np.float64)


N, IN, D, H = 1024, 1024, 512, 4
EPS = 1e-5


def ln(u, g, b):
    mu = u.mean(-1, keepdims=True)
    var = ((u - mu) ** 2).mean(-1, keepdims=True)
    return (u - mu) / np.sqrt(var + EPS) * g + b


def setup_inputs():
    s = mx_kscale(IN)
    return {
        "x": bf(np.random.standard_normal((N, IN)) * s),
        "W1": bf(np.random.standard_normal((IN, D)) / np.sqrt(IN) / s[:, None]),
        "b1": bf(0.3 * np.random.standard_normal(D)),
        "ln1_g": bf(1.0 + 0.1 * np.random.standard_normal(D)),
        "ln1_b": bf(0.1 * np.random.standard_normal(D)),
        "W2": bf(np.random.standard_normal((D, D)) / np.sqrt(D)),
        "b2": bf(0.2 * np.random.standard_normal(D)),
        "ln2_g": bf(1.0 + 0.1 * np.random.standard_normal(D)),
        "ln2_b": bf(0.1 * np.random.standard_normal(D)),
    }


def reference(x, W1, b1, ln1_g, ln1_b, W2, b2, ln2_g, ln2_b):
    z1 = (mxq(f64(x), 1, "e4m3") @ mxq(f64(W1), 0, "e4m3")) + f64(b1)
    h1 = ln(np.maximum(z1, 0.0), f64(ln1_g), f64(ln1_b))
    z2 = (mxq(h1, 1, "e4m3") @ mxq(f64(W2), 0, "e4m3")) + f64(b2) + h1
    return ln(np.maximum(z2, 0.0), f64(ln2_g), f64(ln2_b))

@@ -1,0 +1,257 @@
+import concourse.mybir as mybir
+from concourse.masks import make_identity
+
+F32 = mybir.dt.float32
+BF16 = mybir.dt.bfloat16
+U32 = mybir.dt.uint32
+U8 = mybir.dt.uint8
+FP8X4 = mybir.dt.float8_e4m3fn_x4
+ALU = mybir.AluOpType
+ACT = mybir.ActivationFunctionType
+
+P = 128
+PACK = 4
+K_PASS = P * PACK
+N_TOKENS = 1024
+D_IN = 1024
+D = 512
+TOKEN_TILES = N_TOKENS // P
+PASSES_1 = D_IN // K_PASS
+EPS = 1e-5
+
+FLOPS = 2 * N_TOKENS * D_IN * D + 2 * N_TOKENS * D * D
+
+
+def regroup_and_quantise(nc, stage, raw, codes, scales):
+    grouped = stage.tile([P, D, PACK], BF16, align_bytes=64, tag="w_grouped")
+    nc.vector.tensor_copy(
+        out=grouped[:].rearrange("p (c i) t -> p c t i", i=4),
+        in_=raw.rearrange("p t (c i) -> p c t i", i=4),
+    )
+    nc.vector.quantize_mx(
+        out=codes.bitcast(FP8X4),
+        scales=scales,
+        in_=grouped[:].rearrange("p c t -> p (c t)"),
+    )
+
+
+def relu_and_mean(nc, work, stats, layer, pre):
+    act = work.tile([P, D], F32, tag="act" + layer)
+    total = stats.tile([P, 1], F32, tag="total" + layer)
+    nc.scalar.activation(out=act[:], in_=pre[:], func=ACT.Relu, accum_out=total[:])
+    neg_mean = stats.tile([P, 1], F32, tag="neg_mean" + layer)
+    nc.scalar.mul(out=neg_mean[:], in_=total[:], mul=-1.0 / D)
+    return act, neg_mean
+
+
+def deviation(nc, work, stats, layer, eps_col, act, neg_mean):
+    squares = work.tile([P, D], F32, tag="squares" + layer)
+    sq_dev = stats.tile([P, 1], F32, tag="sq_dev" + layer)
+    nc.scalar.activation(
+        out=squares[:], in_=act[:], func=ACT.Square, bias=neg_mean[:], accum_out=sq_dev[:]
+    )
+    std = stats.tile([P, 1], F32, tag="std" + layer)
+    nc.scalar.activation(out=std[:], in_=sq_dev[:], func=ACT.Sqrt, bias=eps_col[:], scale=1.0 / D)
+    return std
+
+
+def centre_and_gain(nc, work, layer, act, neg_mean, gain):
+    centred = work.tile([P, D], F32, tag="centred" + layer)
+    nc.vector.scalar_tensor_tensor(
+        out=centred[:], in0=act[:], scalar=neg_mean[:], in1=gain[:], op0=ALU.add, op1=ALU.mult
+    )
+    return centred
+
+
+def scale_and_shift(nc, work, stats, layer, centred, std, shifts):
+    rstd = stats.tile([P, 1], F32, tag="rstd" + layer)
+    nc.vector.reciprocal(out=rstd[:], in_=std[:])
+    results = []
+    for n, shift in enumerate(shifts):
+        result = work.tile([P, D], F32, name="normed", tag="normed%d" % n + layer)
+        nc.vector.scalar_tensor_tensor(
+            out=result[:], in0=centred[:], scalar=rstd[:], in1=shift[:], op0=ALU.mult, op1=ALU.add
+        )
+        results.append(result)
+    return results
+
+
+def tile_multiscalegatencoder_pa_kernel(
+    tc, x, W1, b1, ln1_g, ln1_b, W2, b2, ln2_g, ln2_b, out
+):
+    nc = tc.nc
+    with (
+        tc.tile_pool(name="const", bufs=1) as const,
+        tc.tile_pool(name="stage", bufs=2) as stage,
+        tc.tile_pool(name="work", bufs=3) as work,
+        tc.tile_pool(name="stats", bufs=4) as stats,
+        tc.psum_pool(name="psum", bufs=2) as psum,
+        tc.manual_schedule(),
+    ):
+        x_sb = const.tile([P, TOKEN_TILES, D_IN], BF16)
+        w1_raw = const.tile([P, PASSES_1, PACK, D], BF16)
+        w2_raw = const.tile([P, PACK, D], BF16)
+
+        def load_x(i):
+            nc.sync.dma_start(out=x_sb[:, i, :], in_=x[i * P : (i + 1) * P, :])
+
+        load_x(0)
+        for g in range(PASSES_1):
+            nc.sync.dma_start(
+                out=w1_raw[:, g].rearrange("q (u e) c -> q u e c", u=2),
+                in_=W1[g * K_PASS : (g + 1) * K_PASS, :].rearrange(
+                    "(u q e) c -> q u e c", u=2, e=2
+                ),
+            )
+        load_x(1)
+        nc.sync.dma_start(out=w2_raw[:], in_=W2.rearrange("(t p) c -> p t c", p=P))
+        for i in range(2, TOKEN_TILES):
+            load_x(i)
+
+        ident_f32 = const.tile([P, P], F32)
+        make_identity(nc, ident_f32[:])
+        ident_bf16 = const.tile([P, P], BF16)
+        make_identity(nc, ident_bf16[:])
+        eps_col = const.tile([P, 1], F32)
+        nc.vector.memset(eps_col[:], EPS)
+
+        vec_rows = const.tile([P, D], BF16)
+        nc.vector.memset(vec_rows[:], 0.0)
+        row_of = {}
+        for r, (name, vec) in enumerate(
+            [("b1", b1), ("g1", ln1_g), ("s1", ln1_b), ("b2", b2), ("g2", ln2_g), ("s2", ln2_b)]
+        ):
+            nc.scalar.dma_start(out=vec_rows[r : r + 1, :], in_=vec.unsqueeze(0))
+            row_of[name] = r
+        warm = const.tile([P, 1], F32)
+        nc.scalar.sqrt(out=warm[:], in_=eps_col[:])
+
+        def spread(name, rows):
+            bank = psum.tile([P, D], F32, tag="z2")
+            for n, row in enumerate(rows):
+                r = row_of[row]
+                nc.tensor.matmul(
+                    out=bank[:],
+                    lhsT=ident_bf16[:, r : r + 1].to_broadcast([P, P]),
+                    rhs=vec_rows[:],
+                    start=(n == 0),
+                    stop=(n == len(rows) - 1),
+                )
+            full = const.tile([P, D], F32, name=name)
+            nc.scalar.copy(out=full[:], in_=bank[:])
+            return full
+
+        x_grouped, z1, z2, ln1, ln2, h1_b2, h_grouped = {}, {}, {}, {}, {}, {}, {}
+
+        def transpose_x(i):
+            x_words = x_sb[:, i, :].bitcast(F32)
+            xt = psum.tile([P, PASSES_1 * 2, P], F32, tag="xt")
+            for s in range(PASSES_1 * 2):
+                nc.tensor.transpose(xt[:, s, :], x_words[:, s * P : (s + 1) * P], ident_f32[:])
+            grouped = stage.tile([P, PASSES_1 * P * PACK], BF16, align_bytes=64, tag="x_grouped")
+            nc.scalar.copy(
+                out=grouped[:].bitcast(F32).rearrange("p (g r u) -> p g r u", g=PASSES_1, u=2),
+                in_=xt[:].rearrange("p (g u) r -> p g r u", u=2),
+            )
+            x_grouped[i] = grouped
+
+        def first_matmul(i):
+            x_codes = stage.tile([P, PASSES_1 * P], U32, align_bytes=64)
+            x_scales = stage.tile([P, PASSES_1 * P], U8, align_bytes=64)
+            nc.vector.quantize_mx(
+                out=x_codes[:].bitcast(FP8X4), scales=x_scales[:], in_=x_grouped[i][:]
+            )
+            bank = psum.tile([P, D], F32, tag="z1")
+            for g in range(PASSES_1):
+                tokens = slice(g * P, (g + 1) * P)
+                nc.tensor.matmul_mx(
+                    out=bank[:],
+                    lhsT=x_codes[:, tokens].bitcast(FP8X4),
+                    lhsT_scale=x_scales[:, tokens],
+                    rhs=w1_codes[:, g, :].bitcast(FP8X4),
+                    rhs_scale=w1_scales[:, g, :],
+                    start=(g == 0),
+                    stop=(g == PASSES_1 - 1),
+                )
+            z1[i] = bank
+
+        def transpose_h(i, h1):
+            ht = psum.tile([P, PACK, P], F32, tag="ht")
+            for t in range(PACK):
+                nc.tensor.transpose(ht[:, t, :], h1[:, t * P : (t + 1) * P], ident_f32[:])
+            grouped = stage.tile([P, P, PACK], BF16, align_bytes=64, tag="h_grouped")
+            nc.scalar.copy(out=grouped[:], in_=ht[:].rearrange("p t r -> p r t"))
+            h_grouped[i] = grouped
+
+        def second_matmul(i):
+            h_codes = stage.tile([P, P], U32, align_bytes=64)
+            h_scales = stage.tile([P, P], U8, align_bytes=64)
+            nc.vector.quantize_mx(
+                out=h_codes[:].bitcast(FP8X4),
+                scales=h_scales[:],
+                in_=h_grouped[i][:].rearrange("p r t -> p (r t)"),
+            )
+            bank = psum.tile([P, D], F32, tag="z2")
+            nc.tensor.matmul_mx(
+                out=bank[:],
+                lhsT=h_codes[:].bitcast(FP8X4),
+                lhsT_scale=h_scales[:],
+                rhs=w2_codes[:].bitcast(FP8X4),
+                rhs_scale=w2_scales[:],
+                start=True,
+                stop=True,
+            )
+            z2[i] = bank
+
+        def add_and_relu(layer, bank, addend):
+            pre = work.tile([P, D], F32, tag="pre" + layer)
+            nc.vector.tensor_tensor(out=pre[:], in0=bank[:], in1=addend[:], op=ALU.add)
+            return relu_and_mean(nc, work, stats, layer, pre)
+
+        transpose_x(0)
+        transpose_x(1)
+        b1_full = spread("b1_full", ["b1"])
+        g1_full = spread("g1_full", ["g1"])
+        s1_full = spread("s1_full", ["s1"])
+        s1_b2_full = spread("s1_b2_full", ["s1", "b2"])
+        g2_full = spread("g2_full", ["g2"])
+        s2_full = spread("s2_full", ["s2"])
+        w1_codes = const.tile([P, PASSES_1, D], U32, align_bytes=64)
+        w1_scales = const.tile([P, PASSES_1, D], U8, align_bytes=64)
+        for g in range(PASSES_1):
+            regroup_and_quantise(nc, stage, w1_raw[:, g], w1_codes[:, g, :], w1_scales[:, g, :])
+        first_matmul(0)
+        w2_codes = const.tile([P, D], U32, align_bytes=64)
+        w2_scales = const.tile([P, D], U8, align_bytes=64)
+        regroup_and_quantise(nc, stage, w2_raw[:], w2_codes[:], w2_scales[:])
+
+        for i in range(TOKEN_TILES + 1):
+            j = i - 1
+            first = i < TOKEN_TILES
+            second = j >= 0
+            if first:
+                ln1[i] = add_and_relu("1", z1[i], b1_full)
+            if second:
+                ln2[j] = add_and_relu("2", z2[j], h1_b2[j])
+            if i + 1 < TOKEN_TILES:
+                first_matmul(i + 1)
+            if first:
+                act1, neg_mean1 = ln1[i]
+                centred1 = centre_and_gain(nc, work, "1", act1, neg_mean1, g1_full)
+                std1 = deviation(nc, work, stats, "1", eps_col, act1, neg_mean1)
+            if second:
+                act2, neg_mean2 = ln2[j]
+                centred2 = centre_and_gain(nc, work, "2", act2, neg_mean2, g2_full)
+                std2 = deviation(nc, work, stats, "2", eps_col, act2, neg_mean2)
+            if i + 2 < TOKEN_TILES:
+                transpose_x(i + 2)
+            if first:
+                h1, h1_b2[i] = scale_and_shift(
+                    nc, work, stats, "1", centred1, std1, [s1_full, s1_b2_full]
+                )
+                transpose_h(i, h1)
+            if second:
+                (result,) = scale_and_shift(nc, work, stats, "2", centred2, std2, [s2_full])
+                nc.sync.dma_start(out=out[j * P : (j + 1) * P, :], in_=result[:])
+            if first:
+                second_matmul(i)

@@ -15,65 +15,100 @@ K_PASS = P * PACK
 N_TOKENS = 1024
 D_IN = 1024
 D = 512
-TOKEN_TILES = N_TOKENS // P
+TILES = N_TOKENS // P
+HALF = TILES // 2
 PASSES_1 = D_IN // K_PASS
 EPS = 1e-5
 
 FLOPS = 2 * N_TOKENS * D_IN * D + 2 * N_TOKENS * D * D
 
 
-def regroup_and_quantise(nc, stage, raw, codes, scales):
-    grouped = stage.tile([P, D, PACK], BF16, align_bytes=64, tag="w_grouped")
-    nc.vector.tensor_copy(
+def half_tiles(h):
+    return range(h * HALF, (h + 1) * HALF)
+
+
+def half_cols(h):
+    return slice(h * HALF, (h + 1) * HALF)
+
+
+def regroup(copy, grouped, raw):
+    copy(
         out=grouped[:].rearrange("p (c i) t -> p c t i", i=4),
         in_=raw.rearrange("p t (c i) -> p c t i", i=4),
     )
-    nc.vector.quantize_mx(
-        out=codes.bitcast(FP8X4),
-        scales=scales,
-        in_=grouped[:].rearrange("p c t -> p (c t)"),
-    )
 
 
-def relu_and_mean(nc, work, stats, layer, pre):
-    act = work.tile([P, D], F32, tag="act" + layer)
-    total = stats.tile([P, 1], F32, tag="total" + layer)
-    nc.scalar.activation(out=act[:], in_=pre[:], func=ACT.Relu, accum_out=total[:])
-    neg_mean = stats.tile([P, 1], F32, tag="neg_mean" + layer)
-    nc.scalar.mul(out=neg_mean[:], in_=total[:], mul=-1.0 / D)
-    return act, neg_mean
+def quantise(nc, grouped, codes, scales):
+    nc.vector.quantize_mx(out=codes.bitcast(FP8X4), scales=scales, in_=grouped)
 
 
-def deviation(nc, work, stats, layer, eps_col, act, neg_mean):
-    squares = work.tile([P, D], F32, tag="squares" + layer)
-    sq_dev = stats.tile([P, 1], F32, tag="sq_dev" + layer)
+def new_layer_norm(const, layer):
+    names = ["total", "neg_mean", "sq_dev", "std", "rstd"]
+    ln = {n: const.tile([P, TILES], F32, name=n + layer) for n in names}
+    ln["act"] = {}
+    ln["centred"] = {}
+    return ln
+
+
+def relu_and_sum(nc, work, ln, i, pre):
+    act = work.tile([P, D], F32, tag="act", bufs=TILES)
     nc.scalar.activation(
-        out=squares[:], in_=act[:], func=ACT.Square, bias=neg_mean[:], accum_out=sq_dev[:]
+        out=act[:], in_=pre[:], func=ACT.Relu, accum_out=ln["total"][:, i : i + 1]
     )
-    std = stats.tile([P, 1], F32, tag="std" + layer)
-    nc.scalar.activation(out=std[:], in_=sq_dev[:], func=ACT.Sqrt, bias=eps_col[:], scale=1.0 / D)
-    return std
+    ln["act"][i] = act
 
 
-def centre_and_gain(nc, work, layer, act, neg_mean, gain):
-    centred = work.tile([P, D], F32, tag="centred" + layer)
+def negate_means(nc, ln, h):
+    nc.scalar.mul(out=ln["neg_mean"][:, half_cols(h)], in_=ln["total"][:, half_cols(h)], mul=-1.0 / D)
+
+
+def sum_squared_deviations(nc, work, ln, i):
+    squares = work.tile([P, D], F32, tag="squares", bufs=2)
+    nc.scalar.activation(
+        out=squares[:],
+        in_=ln["act"][i][:],
+        func=ACT.Square,
+        bias=ln["neg_mean"][:, i : i + 1],
+        accum_out=ln["sq_dev"][:, i : i + 1],
+    )
+
+
+def standard_deviations(nc, ln, h, eps_col):
+    nc.scalar.activation(
+        out=ln["std"][:, half_cols(h)],
+        in_=ln["sq_dev"][:, half_cols(h)],
+        func=ACT.Sqrt,
+        bias=eps_col[:],
+        scale=1.0 / D,
+    )
+
+
+def centre_and_gain(nc, work, ln, i, gain):
+    centred = work.tile([P, D], F32, tag="centred", bufs=TILES)
     nc.vector.scalar_tensor_tensor(
-        out=centred[:], in0=act[:], scalar=neg_mean[:], in1=gain[:], op0=ALU.add, op1=ALU.mult
+        out=centred[:],
+        in0=ln["act"][i][:],
+        scalar=ln["neg_mean"][:, i : i + 1],
+        in1=gain[:],
+        op0=ALU.add,
+        op1=ALU.mult,
     )
-    return centred
+    ln["centred"][i] = centred
 
 
-def scale_and_shift(nc, work, stats, layer, centred, std, shifts):
-    rstd = stats.tile([P, 1], F32, tag="rstd" + layer)
-    nc.vector.reciprocal(out=rstd[:], in_=std[:])
-    results = []
-    for n, shift in enumerate(shifts):
-        result = work.tile([P, D], F32, name="normed", tag="normed%d" % n + layer)
-        nc.vector.scalar_tensor_tensor(
-            out=result[:], in0=centred[:], scalar=rstd[:], in1=shift[:], op0=ALU.mult, op1=ALU.add
-        )
-        results.append(result)
-    return results
+def invert_deviations(nc, ln, h):
+    nc.vector.reciprocal(out=ln["rstd"][:, half_cols(h)], in_=ln["std"][:, half_cols(h)])
+
+
+def scale_and_shift(nc, ln, i, shift, result):
+    nc.vector.scalar_tensor_tensor(
+        out=result[:],
+        in0=ln["centred"][i][:],
+        scalar=ln["rstd"][:, i : i + 1],
+        in1=shift[:],
+        op0=ALU.mult,
+        op1=ALU.add,
+    )
 
 
 def tile_multiscalegatencoder_pa_kernel(
@@ -82,73 +117,95 @@ def tile_multiscalegatencoder_pa_kernel(
     nc = tc.nc
     with (
         tc.tile_pool(name="const", bufs=1) as const,
-        tc.tile_pool(name="stage", bufs=2) as stage,
-        tc.tile_pool(name="work", bufs=3) as work,
-        tc.tile_pool(name="stats", bufs=4) as stats,
-        tc.psum_pool(name="psum", bufs=2) as psum,
+        tc.tile_pool(name="work", bufs=4) as work,
+        tc.psum_pool(name="psum", bufs=4) as psum,
         tc.manual_schedule(),
     ):
-        x_sb = const.tile([P, TOKEN_TILES, D_IN], BF16)
+        x_sb = const.tile([P, TILES, D_IN], BF16)
         w1_raw = const.tile([P, PASSES_1, PACK, D], BF16)
         w2_raw = const.tile([P, PACK, D], BF16)
 
         def load_x(i):
             nc.sync.dma_start(out=x_sb[:, i, :], in_=x[i * P : (i + 1) * P, :])
 
-        load_x(0)
-        for g in range(PASSES_1):
+        def load_w1(g):
             nc.sync.dma_start(
                 out=w1_raw[:, g].rearrange("q (u e) c -> q u e c", u=2),
                 in_=W1[g * K_PASS : (g + 1) * K_PASS, :].rearrange(
                     "(u q e) c -> q u e c", u=2, e=2
                 ),
             )
-        load_x(1)
-        nc.sync.dma_start(out=w2_raw[:], in_=W2.rearrange("(t p) c -> p t c", p=P))
-        for i in range(2, TOKEN_TILES):
-            load_x(i)
 
-        ident_f32 = const.tile([P, P], F32)
-        make_identity(nc, ident_f32[:])
+        early_rows = const.tile([P, D], BF16)
+        nc.vector.memset(early_rows[:], 0.0)
+        late_rows = const.tile([P, D], BF16)
+        nc.vector.memset(late_rows[:], 0.0)
+        place_of = {
+            "b1": (early_rows, 0),
+            "g1": (early_rows, 1),
+            "s1": (early_rows, 2),
+            "b2": (late_rows, 0),
+            "g2": (late_rows, 1),
+            "s2": (late_rows, 2),
+        }
+
+        def load_vector(queue, name, vec):
+            rows, r = place_of[name]
+            queue.dma_start(out=rows[r : r + 1, :], in_=vec.unsqueeze(0))
+
+        load_vector(nc.scalar, "b1", b1)
+        load_vector(nc.scalar, "g1", ln1_g)
+        load_vector(nc.scalar, "s1", ln1_b)
+        load_w1(0)
+        load_x(0)
+        load_w1(1)
+        for i in range(1, TILES):
+            load_x(i)
+        load_vector(nc.sync, "b2", b2)
+        nc.sync.dma_start(out=w2_raw[:], in_=W2.rearrange("(t p) c -> p t c", p=P))
+        load_vector(nc.sync, "g2", ln2_g)
+        load_vector(nc.sync, "s2", ln2_b)
+
         ident_bf16 = const.tile([P, P], BF16)
         make_identity(nc, ident_bf16[:])
+        ident_f32 = const.tile([P, P], F32)
+        make_identity(nc, ident_f32[:])
         eps_col = const.tile([P, 1], F32)
         nc.vector.memset(eps_col[:], EPS)
-
-        vec_rows = const.tile([P, D], BF16)
-        nc.vector.memset(vec_rows[:], 0.0)
-        row_of = {}
-        for r, (name, vec) in enumerate(
-            [("b1", b1), ("g1", ln1_g), ("s1", ln1_b), ("b2", b2), ("g2", ln2_g), ("s2", ln2_b)]
-        ):
-            nc.scalar.dma_start(out=vec_rows[r : r + 1, :], in_=vec.unsqueeze(0))
-            row_of[name] = r
         warm = const.tile([P, 1], F32)
         nc.scalar.sqrt(out=warm[:], in_=eps_col[:])
 
-        def spread(name, rows):
-            bank = psum.tile([P, D], F32, tag="z2")
-            for n, row in enumerate(rows):
-                r = row_of[row]
+        def spread(name, vectors):
+            bank = psum.tile([P, D], F32, tag="plain")
+            for n, vector in enumerate(vectors):
+                rows, r = place_of[vector]
                 nc.tensor.matmul(
                     out=bank[:],
                     lhsT=ident_bf16[:, r : r + 1].to_broadcast([P, P]),
-                    rhs=vec_rows[:],
+                    rhs=rows[:],
                     start=(n == 0),
-                    stop=(n == len(rows) - 1),
+                    stop=(n == len(vectors) - 1),
                 )
             full = const.tile([P, D], F32, name=name)
             nc.scalar.copy(out=full[:], in_=bank[:])
             return full
 
-        x_grouped, z1, z2, ln1, ln2, h1_b2, h_grouped = {}, {}, {}, {}, {}, {}, {}
+        x_grouped, z1, z2, h1_b2, h_grouped = {}, {}, {}, {}, {}
+        ln1 = new_layer_norm(const, "1")
+        ln2 = new_layer_norm(const, "2")
+        w1_codes = const.tile([P, PASSES_1, D], U32, align_bytes=64)
+        w1_scales = const.tile([P, PASSES_1, D], U8, align_bytes=64)
+        w2_codes = const.tile([P, D], U32, align_bytes=64)
+        w2_scales = const.tile([P, D], U8, align_bytes=64)
 
         def transpose_x(i):
             x_words = x_sb[:, i, :].bitcast(F32)
-            xt = psum.tile([P, PASSES_1 * 2, P], F32, tag="xt")
+            xt = psum.tile([P, PASSES_1 * 2, P], F32, tag="plain")
             for s in range(PASSES_1 * 2):
                 nc.tensor.transpose(xt[:, s, :], x_words[:, s * P : (s + 1) * P], ident_f32[:])
-            grouped = stage.tile([P, PASSES_1 * P * PACK], BF16, align_bytes=64, tag="x_grouped")
+            grouped = work.tile(
+                [P, PASSES_1 * P * PACK], BF16, align_bytes=64, tag="x_grouped", bufs=6
+            )
             nc.scalar.copy(
                 out=grouped[:].bitcast(F32).rearrange("p (g r u) -> p g r u", g=PASSES_1, u=2),
                 in_=xt[:].rearrange("p (g u) r -> p g r u", u=2),
@@ -156,12 +213,10 @@ def tile_multiscalegatencoder_pa_kernel(
             x_grouped[i] = grouped
 
         def first_matmul(i):
-            x_codes = stage.tile([P, PASSES_1 * P], U32, align_bytes=64)
-            x_scales = stage.tile([P, PASSES_1 * P], U8, align_bytes=64)
-            nc.vector.quantize_mx(
-                out=x_codes[:].bitcast(FP8X4), scales=x_scales[:], in_=x_grouped[i][:]
-            )
-            bank = psum.tile([P, D], F32, tag="z1")
+            x_codes = work.tile([P, PASSES_1 * P], U32, align_bytes=64)
+            x_scales = work.tile([P, PASSES_1 * P], U8, align_bytes=64)
+            quantise(nc, x_grouped[i][:], x_codes[:], x_scales[:])
+            bank = psum.tile([P, D], F32, tag="mx")
             for g in range(PASSES_1):
                 tokens = slice(g * P, (g + 1) * P)
                 nc.tensor.matmul_mx(
@@ -175,23 +230,29 @@ def tile_multiscalegatencoder_pa_kernel(
                 )
             z1[i] = bank
 
-        def transpose_h(i, h1):
-            ht = psum.tile([P, PACK, P], F32, tag="ht")
+        def add_to_bank(bank, addend):
+            pre = work.tile([P, D], F32, tag="pre", bufs=5)
+            nc.vector.tensor_tensor(out=pre[:], in0=bank[:], in1=addend[:], op=ALU.add)
+            return pre
+
+        def finish_first_norm(i):
+            h1 = work.tile([P, D], F32)
+            scale_and_shift(nc, ln1, i, s1_full, h1)
+            ht = psum.tile([P, PACK, P], F32, tag="plain")
             for t in range(PACK):
                 nc.tensor.transpose(ht[:, t, :], h1[:, t * P : (t + 1) * P], ident_f32[:])
-            grouped = stage.tile([P, P, PACK], BF16, align_bytes=64, tag="h_grouped")
+            return ht
+
+        def round_h(i, ht):
+            grouped = work.tile([P, P, PACK], BF16, align_bytes=64, tag="h_grouped", bufs=TILES)
             nc.scalar.copy(out=grouped[:], in_=ht[:].rearrange("p t r -> p r t"))
             h_grouped[i] = grouped
 
         def second_matmul(i):
-            h_codes = stage.tile([P, P], U32, align_bytes=64)
-            h_scales = stage.tile([P, P], U8, align_bytes=64)
-            nc.vector.quantize_mx(
-                out=h_codes[:].bitcast(FP8X4),
-                scales=h_scales[:],
-                in_=h_grouped[i][:].rearrange("p r t -> p (r t)"),
-            )
-            bank = psum.tile([P, D], F32, tag="z2")
+            h_codes = work.tile([P, P], U32, align_bytes=64, bufs=5)
+            h_scales = work.tile([P, P], U8, align_bytes=64, bufs=5)
+            quantise(nc, h_grouped[i][:].rearrange("p r t -> p (r t)"), h_codes[:], h_scales[:])
+            bank = psum.tile([P, D], F32, tag="mx")
             nc.tensor.matmul_mx(
                 out=bank[:],
                 lhsT=h_codes[:].bitcast(FP8X4),
@@ -203,55 +264,72 @@ def tile_multiscalegatencoder_pa_kernel(
             )
             z2[i] = bank
 
-        def add_and_relu(layer, bank, addend):
-            pre = work.tile([P, D], F32, tag="pre" + layer)
-            nc.vector.tensor_tensor(out=pre[:], in0=bank[:], in1=addend[:], op=ALU.add)
-            return relu_and_mean(nc, work, stats, layer, pre)
-
-        transpose_x(0)
-        transpose_x(1)
         b1_full = spread("b1_full", ["b1"])
         g1_full = spread("g1_full", ["g1"])
         s1_full = spread("s1_full", ["s1"])
+        transpose_x(0)
+        transpose_x(1)
+        transpose_x(2)
+        transpose_x(3)
+        for g in range(PASSES_1):
+            w_grouped = work.tile([P, D, PACK], BF16, align_bytes=64, tag="w_grouped", bufs=2)
+            regroup(nc.vector.tensor_copy, w_grouped, w1_raw[:, g])
+            quantise(
+                nc, w_grouped[:].rearrange("p c t -> p (c t)"), w1_codes[:, g, :], w1_scales[:, g, :]
+            )
+        first_matmul(0)
+        transpose_x(4)
+        first_matmul(1)
+        transpose_x(5)
+
+        for i in range(TILES):
+            pre = add_to_bank(z1[i], b1_full)
+            if i + 2 < TILES:
+                first_matmul(i + 2)
+            if i + 6 < TILES:
+                transpose_x(i + 6)
+            relu_and_sum(nc, work, ln1, i, pre)
+            if i == HALF - 1:
+                negate_means(nc, ln1, 0)
+        negate_means(nc, ln1, 1)
+
+        for h in range(2):
+            for i in half_tiles(h):
+                centre_and_gain(nc, work, ln1, i, g1_full)
+                sum_squared_deviations(nc, work, ln1, i)
+            standard_deviations(nc, ln1, h, eps_col)
+
         s1_b2_full = spread("s1_b2_full", ["s1", "b2"])
+        w2_grouped = work.tile([P, D, PACK], BF16, align_bytes=64, tag="w_grouped", bufs=2)
+        regroup(nc.scalar.copy, w2_grouped, w2_raw[:])
+
+        for h in range(2):
+            invert_deviations(nc, ln1, h)
+            banks = {i: finish_first_norm(i) for i in half_tiles(h)}
+            for i in half_tiles(h):
+                round_h(i, banks[i])
         g2_full = spread("g2_full", ["g2"])
         s2_full = spread("s2_full", ["s2"])
-        w1_codes = const.tile([P, PASSES_1, D], U32, align_bytes=64)
-        w1_scales = const.tile([P, PASSES_1, D], U8, align_bytes=64)
-        for g in range(PASSES_1):
-            regroup_and_quantise(nc, stage, w1_raw[:, g], w1_codes[:, g, :], w1_scales[:, g, :])
-        first_matmul(0)
-        w2_codes = const.tile([P, D], U32, align_bytes=64)
-        w2_scales = const.tile([P, D], U8, align_bytes=64)
-        regroup_and_quantise(nc, stage, w2_raw[:], w2_codes[:], w2_scales[:])
+        for i in range(TILES):
+            h1_b2[i] = work.tile([P, D], F32, name="h1_b2", bufs=TILES)
+            scale_and_shift(nc, ln1, i, s1_b2_full, h1_b2[i])
 
-        for i in range(TOKEN_TILES + 1):
-            j = i - 1
-            first = i < TOKEN_TILES
-            second = j >= 0
-            if first:
-                ln1[i] = add_and_relu("1", z1[i], b1_full)
-            if second:
-                ln2[j] = add_and_relu("2", z2[j], h1_b2[j])
-            if i + 1 < TOKEN_TILES:
-                first_matmul(i + 1)
-            if first:
-                act1, neg_mean1 = ln1[i]
-                centred1 = centre_and_gain(nc, work, "1", act1, neg_mean1, g1_full)
-                std1 = deviation(nc, work, stats, "1", eps_col, act1, neg_mean1)
-            if second:
-                act2, neg_mean2 = ln2[j]
-                centred2 = centre_and_gain(nc, work, "2", act2, neg_mean2, g2_full)
-                std2 = deviation(nc, work, stats, "2", eps_col, act2, neg_mean2)
-            if i + 2 < TOKEN_TILES:
-                transpose_x(i + 2)
-            if first:
-                h1, h1_b2[i] = scale_and_shift(
-                    nc, work, stats, "1", centred1, std1, [s1_full, s1_b2_full]
-                )
-                transpose_h(i, h1)
-            if second:
-                (result,) = scale_and_shift(nc, work, stats, "2", centred2, std2, [s2_full])
-                nc.sync.dma_start(out=out[j * P : (j + 1) * P, :], in_=result[:])
-            if first:
+        quantise(nc, w2_grouped[:].rearrange("p c t -> p (c t)"), w2_codes[:], w2_scales[:])
+        for h in range(2):
+            for i in half_tiles(h):
                 second_matmul(i)
+            for i in half_tiles(h):
+                pre = add_to_bank(z2[i], h1_b2[i])
+                relu_and_sum(nc, work, ln2, i, pre)
+            negate_means(nc, ln2, h)
+        for h in range(2):
+            for i in half_tiles(h):
+                centre_and_gain(nc, work, ln2, i, g2_full)
+                sum_squared_deviations(nc, work, ln2, i)
+            standard_deviations(nc, ln2, h, eps_col)
+        for h in range(2):
+            invert_deviations(nc, ln2, h)
+            for i in half_tiles(h):
+                result = work.tile([P, D], F32)
+                scale_and_shift(nc, ln2, i, s2_full, result)
+                nc.sync.dma_start(out=out[i * P : (i + 1) * P, :], in_=result[:])

@@ -153,10 +153,10 @@ def tile_multiscalegatencoder_pa_kernel(
             rows, r = place_of[name]
             queue.dma_start(out=rows[r : r + 1, :], in_=vec.unsqueeze(0))
 
-        load_vector(nc.scalar, "b1", b1)
-        load_vector(nc.scalar, "g1", ln1_g)
-        load_vector(nc.scalar, "s1", ln1_b)
         load_w1(0)
+        load_vector(nc.sync, "b1", b1)
+        load_vector(nc.sync, "g1", ln1_g)
+        load_vector(nc.sync, "s1", ln1_b)
         load_x(0)
         load_w1(1)
         for i in range(1, TILES):
@@ -175,8 +175,8 @@ def tile_multiscalegatencoder_pa_kernel(
         warm = const.tile([P, 1], F32)
         nc.scalar.sqrt(out=warm[:], in_=eps_col[:])
 
-        def spread(name, vectors):
-            bank = psum.tile([P, D], F32, tag="plain")
+        def spread(vectors, tag):
+            bank = psum.tile([P, D], F32, tag=tag)
             for n, vector in enumerate(vectors):
                 rows, r = place_of[vector]
                 nc.tensor.matmul(
@@ -186,11 +186,14 @@ def tile_multiscalegatencoder_pa_kernel(
                     start=(n == 0),
                     stop=(n == len(vectors) - 1),
                 )
+            return bank
+
+        def keep(copy, name, bank):
             full = const.tile([P, D], F32, name=name)
-            nc.scalar.copy(out=full[:], in_=bank[:])
+            copy(out=full[:], in_=bank[:])
             return full
 
-        x_grouped, z1, z2, h1_b2, h_grouped = {}, {}, {}, {}, {}
+        x_grouped, x_mx, z1, z2, h1_b2, h_grouped = {}, {}, {}, {}, {}, {}
         ln1 = new_layer_norm(const, "1")
         ln2 = new_layer_norm(const, "2")
         w1_codes = const.tile([P, PASSES_1, D], U32, align_bytes=64)
@@ -212,10 +215,14 @@ def tile_multiscalegatencoder_pa_kernel(
             )
             x_grouped[i] = grouped
 
+        def quantise_x(i):
+            codes = work.tile([P, PASSES_1 * P], U32, align_bytes=64, tag="x_codes")
+            scales = work.tile([P, PASSES_1 * P], U8, align_bytes=64, tag="x_scales")
+            quantise(nc, x_grouped[i][:], codes[:], scales[:])
+            x_mx[i] = (codes, scales)
+
         def first_matmul(i):
-            x_codes = work.tile([P, PASSES_1 * P], U32, align_bytes=64)
-            x_scales = work.tile([P, PASSES_1 * P], U8, align_bytes=64)
-            quantise(nc, x_grouped[i][:], x_codes[:], x_scales[:])
+            x_codes, x_scales = x_mx[i]
             bank = psum.tile([P, D], F32, tag="mx")
             for g in range(PASSES_1):
                 tokens = slice(g * P, (g + 1) * P)
@@ -264,31 +271,38 @@ def tile_multiscalegatencoder_pa_kernel(
             )
             z2[i] = bank
 
-        b1_full = spread("b1_full", ["b1"])
-        g1_full = spread("g1_full", ["g1"])
-        s1_full = spread("s1_full", ["s1"])
-        transpose_x(0)
-        transpose_x(1)
-        transpose_x(2)
-        transpose_x(3)
+        b1_bank = spread(["b1"], "mx")
+        g1_bank = spread(["g1"], "mx")
+        s1_bank = spread(["s1"], "mx")
+        b1_full = keep(nc.scalar.copy, "b1_full", b1_bank)
+        for i in range(4):
+            transpose_x(i)
         for g in range(PASSES_1):
             w_grouped = work.tile([P, D, PACK], BF16, align_bytes=64, tag="w_grouped", bufs=2)
             regroup(nc.vector.tensor_copy, w_grouped, w1_raw[:, g])
             quantise(
                 nc, w_grouped[:].rearrange("p c t -> p (c t)"), w1_codes[:, g, :], w1_scales[:, g, :]
             )
+        quantise_x(0)
+        quantise_x(1)
         first_matmul(0)
-        transpose_x(4)
+        g1_full = keep(nc.vector.tensor_copy, "g1_full", g1_bank)
+        s1_full = keep(nc.vector.tensor_copy, "s1_full", s1_bank)
         first_matmul(1)
+        transpose_x(4)
         transpose_x(5)
 
         for i in range(TILES):
             pre = add_to_bank(z1[i], b1_full)
-            if i + 2 < TILES:
-                first_matmul(i + 2)
-            if i + 6 < TILES:
-                transpose_x(i + 6)
+            ahead = [k for k in (i + 2, i + 3) if i % 2 == 0 and k < TILES]
+            for k in ahead:
+                quantise_x(k)
+            for k in ahead:
+                first_matmul(k)
             relu_and_sum(nc, work, ln1, i, pre)
+            for k in ahead:
+                if k + 4 < TILES:
+                    transpose_x(k + 4)
             if i == HALF - 1:
                 negate_means(nc, ln1, 0)
         negate_means(nc, ln1, 1)
@@ -299,37 +313,56 @@ def tile_multiscalegatencoder_pa_kernel(
                 sum_squared_deviations(nc, work, ln1, i)
             standard_deviations(nc, ln1, h, eps_col)
 
-        s1_b2_full = spread("s1_b2_full", ["s1", "b2"])
+        s1_b2_full = keep(nc.scalar.copy, "s1_b2_full", spread(["s1", "b2"], "plain"))
         w2_grouped = work.tile([P, D, PACK], BF16, align_bytes=64, tag="w_grouped", bufs=2)
         regroup(nc.scalar.copy, w2_grouped, w2_raw[:])
 
-        for h in range(2):
+        def h1_and_transposes(h):
             invert_deviations(nc, ln1, h)
-            banks = {i: finish_first_norm(i) for i in half_tiles(h)}
-            for i in half_tiles(h):
-                round_h(i, banks[i])
-        g2_full = spread("g2_full", ["g2"])
-        s2_full = spread("s2_full", ["s2"])
-        for i in range(TILES):
-            h1_b2[i] = work.tile([P, D], F32, name="h1_b2", bufs=TILES)
-            scale_and_shift(nc, ln1, i, s1_b2_full, h1_b2[i])
+            return {i: finish_first_norm(i) for i in half_tiles(h)}
 
-        quantise(nc, w2_grouped[:].rearrange("p c t -> p (c t)"), w2_codes[:], w2_scales[:])
-        for h in range(2):
+        def residual_and_second_matmul(h):
+            for i in half_tiles(h):
+                h1_b2[i] = work.tile([P, D], F32, name="h1_b2", bufs=TILES)
+                scale_and_shift(nc, ln1, i, s1_b2_full, h1_b2[i])
             for i in half_tiles(h):
                 second_matmul(i)
+
+        def add_residual_and_relu(h):
             for i in half_tiles(h):
-                pre = add_to_bank(z2[i], h1_b2[i])
-                relu_and_sum(nc, work, ln2, i, pre)
+                pre2 = add_to_bank(z2[i], h1_b2[i])
+                relu_and_sum(nc, work, ln2, i, pre2)
             negate_means(nc, ln2, h)
-        for h in range(2):
-            for i in half_tiles(h):
-                centre_and_gain(nc, work, ln2, i, g2_full)
-                sum_squared_deviations(nc, work, ln2, i)
-            standard_deviations(nc, ln2, h, eps_col)
-        for h in range(2):
+
+        def store_second_norm(h):
             invert_deviations(nc, ln2, h)
             for i in half_tiles(h):
                 result = work.tile([P, D], F32)
                 scale_and_shift(nc, ln2, i, s2_full, result)
                 nc.sync.dma_start(out=out[i * P : (i + 1) * P, :], in_=result[:])
+
+        banks = h1_and_transposes(0)
+        for i in half_tiles(0):
+            round_h(i, banks[i])
+        banks = h1_and_transposes(1)
+        quantise(nc, w2_grouped[:].rearrange("p c t -> p (c t)"), w2_codes[:], w2_scales[:])
+
+        residual_and_second_matmul(0)
+        for i in half_tiles(1):
+            round_h(i, banks[i])
+        g2_full = keep(nc.scalar.copy, "g2_full", spread(["g2"], "plain"))
+        s2_full = keep(nc.scalar.copy, "s2_full", spread(["s2"], "plain"))
+        add_residual_and_relu(0)
+        residual_and_second_matmul(1)
+        for i in half_tiles(0):
+            sum_squared_deviations(nc, work, ln2, i)
+        standard_deviations(nc, ln2, 0, eps_col)
+        add_residual_and_relu(1)
+        for i in half_tiles(0):
+            centre_and_gain(nc, work, ln2, i, g2_full)
+        store_second_norm(0)
+        for i in half_tiles(1):
+            centre_and_gain(nc, work, ln2, i, g2_full)
+            sum_squared_deviations(nc, work, ln2, i)
+        standard_deviations(nc, ln2, 1, eps_col)
+        store_second_norm(1)

@@ -19,6 +19,8 @@ TILES = N_TOKENS // P
 HALF = TILES // 2
 PASSES_1 = D_IN // K_PASS
 EPS = 1e-5
+X_AHEAD = 6
+MX_AHEAD = 3
 
 FLOPS = 2 * N_TOKENS * D_IN * D + 2 * N_TOKENS * D * D
 
@@ -43,7 +45,7 @@ def quantise(nc, grouped, codes, scales):
 
 
 def new_layer_norm(const, layer):
-    names = ["total", "neg_mean", "sq_dev", "std", "rstd"]
+    names = ["total", "neg_mean", "sq_dev", "rstd"]
     ln = {n: const.tile([P, TILES], F32, name=n + layer) for n in names}
     ln["act"] = {}
     ln["centred"] = {}
@@ -73,11 +75,11 @@ def sum_squared_deviations(nc, work, ln, i):
     )
 
 
-def standard_deviations(nc, ln, h, eps_col):
+def inverse_deviations(nc, ln, h, eps_col):
     nc.scalar.activation(
-        out=ln["std"][:, half_cols(h)],
+        out=ln["rstd"][:, half_cols(h)],
         in_=ln["sq_dev"][:, half_cols(h)],
-        func=ACT.Sqrt,
+        func=ACT.Abs_reciprocal_sqrt,
         bias=eps_col[:],
         scale=1.0 / D,
     )
@@ -94,10 +96,6 @@ def centre_and_gain(nc, work, ln, i, gain):
         op1=ALU.mult,
     )
     ln["centred"][i] = centred
-
-
-def invert_deviations(nc, ln, h):
-    nc.vector.reciprocal(out=ln["rstd"][:, half_cols(h)], in_=ln["std"][:, half_cols(h)])
 
 
 def scale_and_shift(nc, ln, i, shift, result):
@@ -136,35 +134,22 @@ def tile_multiscalegatencoder_pa_kernel(
                 ),
             )
 
-        early_rows = const.tile([P, D], BF16)
-        nc.vector.memset(early_rows[:], 0.0)
-        late_rows = const.tile([P, D], BF16)
-        nc.vector.memset(late_rows[:], 0.0)
-        place_of = {
-            "b1": (early_rows, 0),
-            "g1": (early_rows, 1),
-            "s1": (early_rows, 2),
-            "b2": (late_rows, 0),
-            "g2": (late_rows, 1),
-            "s2": (late_rows, 2),
-        }
-
-        def load_vector(queue, name, vec):
-            rows, r = place_of[name]
-            queue.dma_start(out=rows[r : r + 1, :], in_=vec.unsqueeze(0))
+        vec_rows = const.tile([P, D], BF16)
+        nc.vector.memset(vec_rows[:], 0.0)
 
         load_w1(0)
-        load_vector(nc.sync, "b1", b1)
-        load_vector(nc.sync, "g1", ln1_g)
-        load_vector(nc.sync, "s1", ln1_b)
+        for r, vec in enumerate([b1, ln1_g, ln1_b]):
+            nc.sync.dma_start(out=vec_rows[r : r + 1, :], in_=vec.unsqueeze(0))
         load_x(0)
         load_w1(1)
         for i in range(1, TILES):
             load_x(i)
-        load_vector(nc.sync, "b2", b2)
         nc.sync.dma_start(out=w2_raw[:], in_=W2.rearrange("(t p) c -> p t c", p=P))
-        load_vector(nc.sync, "g2", ln2_g)
-        load_vector(nc.sync, "s2", ln2_b)
+        b2_full = const.tile([P, D], BF16)
+        g2_full = const.tile([P, D], BF16)
+        s2_full = const.tile([P, D], BF16)
+        for full, vec in [(b2_full, b2), (g2_full, ln2_g), (s2_full, ln2_b)]:
+            nc.sync.dma_start(out=full[:], in_=vec.partition_broadcast(P))
 
         ident_bf16 = const.tile([P, P], BF16)
         make_identity(nc, ident_bf16[:])
@@ -173,19 +158,17 @@ def tile_multiscalegatencoder_pa_kernel(
         eps_col = const.tile([P, 1], F32)
         nc.vector.memset(eps_col[:], EPS)
         warm = const.tile([P, 1], F32)
-        nc.scalar.sqrt(out=warm[:], in_=eps_col[:])
+        nc.scalar.activation(out=warm[:], in_=eps_col[:], func=ACT.Abs_reciprocal_sqrt)
 
-        def spread(vectors, tag):
-            bank = psum.tile([P, D], F32, tag=tag)
-            for n, vector in enumerate(vectors):
-                rows, r = place_of[vector]
-                nc.tensor.matmul(
-                    out=bank[:],
-                    lhsT=ident_bf16[:, r : r + 1].to_broadcast([P, P]),
-                    rhs=rows[:],
-                    start=(n == 0),
-                    stop=(n == len(vectors) - 1),
-                )
+        def spread(r):
+            bank = psum.tile([P, D], F32, tag="mx")
+            nc.tensor.matmul(
+                out=bank[:],
+                lhsT=ident_bf16[:, r : r + 1].to_broadcast([P, P]),
+                rhs=vec_rows[:],
+                start=True,
+                stop=True,
+            )
             return bank
 
         def keep(copy, name, bank):
@@ -193,7 +176,7 @@ def tile_multiscalegatencoder_pa_kernel(
             copy(out=full[:], in_=bank[:])
             return full
 
-        x_grouped, x_mx, z1, z2, h1_b2, h_grouped = {}, {}, {}, {}, {}, {}
+        x_grouped, x_mx, z1, z2, h1, h1_b2, h_grouped = {}, {}, {}, {}, {}, {}, {}
         ln1 = new_layer_norm(const, "1")
         ln2 = new_layer_norm(const, "2")
         w1_codes = const.tile([P, PASSES_1, D], U32, align_bytes=64)
@@ -243,11 +226,11 @@ def tile_multiscalegatencoder_pa_kernel(
             return pre
 
         def finish_first_norm(i):
-            h1 = work.tile([P, D], F32)
-            scale_and_shift(nc, ln1, i, s1_full, h1)
+            h1[i] = work.tile([P, D], F32, name="h1", bufs=TILES)
+            scale_and_shift(nc, ln1, i, s1_full, h1[i])
             ht = psum.tile([P, PACK, P], F32, tag="plain")
             for t in range(PACK):
-                nc.tensor.transpose(ht[:, t, :], h1[:, t * P : (t + 1) * P], ident_f32[:])
+                nc.tensor.transpose(ht[:, t, :], h1[i][:, t * P : (t + 1) * P], ident_f32[:])
             return ht
 
         def round_h(i, ht):
@@ -271,38 +254,39 @@ def tile_multiscalegatencoder_pa_kernel(
             )
             z2[i] = bank
 
-        b1_bank = spread(["b1"], "mx")
-        g1_bank = spread(["g1"], "mx")
-        s1_bank = spread(["s1"], "mx")
-        b1_full = keep(nc.scalar.copy, "b1_full", b1_bank)
-        for i in range(4):
-            transpose_x(i)
+        b1_bank = spread(0)
+        g1_bank = spread(1)
+        s1_bank = spread(2)
+        transpose_x(0)
         for g in range(PASSES_1):
             w_grouped = work.tile([P, D, PACK], BF16, align_bytes=64, tag="w_grouped", bufs=2)
             regroup(nc.vector.tensor_copy, w_grouped, w1_raw[:, g])
             quantise(
                 nc, w_grouped[:].rearrange("p c t -> p (c t)"), w1_codes[:, g, :], w1_scales[:, g, :]
             )
+        transpose_x(1)
+        transpose_x(2)
+        b1_full = keep(nc.scalar.copy, "b1_full", b1_bank)
+        for i in range(3, X_AHEAD):
+            transpose_x(i)
         quantise_x(0)
-        quantise_x(1)
         first_matmul(0)
         g1_full = keep(nc.vector.tensor_copy, "g1_full", g1_bank)
-        s1_full = keep(nc.vector.tensor_copy, "s1_full", s1_bank)
+        quantise_x(1)
         first_matmul(1)
-        transpose_x(4)
-        transpose_x(5)
+        s1_full = keep(nc.vector.tensor_copy, "s1_full", s1_bank)
+        for i in range(2, MX_AHEAD):
+            quantise_x(i)
+            first_matmul(i)
 
         for i in range(TILES):
             pre = add_to_bank(z1[i], b1_full)
-            ahead = [k for k in (i + 2, i + 3) if i % 2 == 0 and k < TILES]
-            for k in ahead:
-                quantise_x(k)
-            for k in ahead:
-                first_matmul(k)
+            if i + X_AHEAD < TILES:
+                transpose_x(i + X_AHEAD)
+            if i + MX_AHEAD < TILES:
+                quantise_x(i + MX_AHEAD)
+                first_matmul(i + MX_AHEAD)
             relu_and_sum(nc, work, ln1, i, pre)
-            for k in ahead:
-                if k + 4 < TILES:
-                    transpose_x(k + 4)
             if i == HALF - 1:
                 negate_means(nc, ln1, 0)
         negate_means(nc, ln1, 1)
@@ -311,22 +295,14 @@ def tile_multiscalegatencoder_pa_kernel(
             for i in half_tiles(h):
                 centre_and_gain(nc, work, ln1, i, g1_full)
                 sum_squared_deviations(nc, work, ln1, i)
-            standard_deviations(nc, ln1, h, eps_col)
+            inverse_deviations(nc, ln1, h, eps_col)
 
-        s1_b2_full = keep(nc.scalar.copy, "s1_b2_full", spread(["s1", "b2"], "plain"))
         w2_grouped = work.tile([P, D, PACK], BF16, align_bytes=64, tag="w_grouped", bufs=2)
         regroup(nc.scalar.copy, w2_grouped, w2_raw[:])
 
-        def h1_and_transposes(h):
-            invert_deviations(nc, ln1, h)
-            return {i: finish_first_norm(i) for i in half_tiles(h)}
-
-        def residual_and_second_matmul(h):
-            for i in half_tiles(h):
-                h1_b2[i] = work.tile([P, D], F32, name="h1_b2", bufs=TILES)
-                scale_and_shift(nc, ln1, i, s1_b2_full, h1_b2[i])
-            for i in half_tiles(h):
-                second_matmul(i)
+        def add_b2(i):
+            h1_b2[i] = work.tile([P, D], F32, name="h1_b2", bufs=TILES)
+            nc.vector.tensor_tensor(out=h1_b2[i][:], in0=h1[i][:], in1=b2_full[:], op=ALU.add)
 
         def add_residual_and_relu(h):
             for i in half_tiles(h):
@@ -335,34 +311,40 @@ def tile_multiscalegatencoder_pa_kernel(
             negate_means(nc, ln2, h)
 
         def store_second_norm(h):
-            invert_deviations(nc, ln2, h)
             for i in half_tiles(h):
                 result = work.tile([P, D], F32)
                 scale_and_shift(nc, ln2, i, s2_full, result)
                 nc.sync.dma_start(out=out[i * P : (i + 1) * P, :], in_=result[:])
 
-        banks = h1_and_transposes(0)
-        for i in half_tiles(0):
+        first, second = list(half_tiles(0)), list(half_tiles(1))
+        banks = {i: finish_first_norm(i) for i in first}
+        for i in first:
             round_h(i, banks[i])
-        banks = h1_and_transposes(1)
-        quantise(nc, w2_grouped[:].rearrange("p c t -> p (c t)"), w2_codes[:], w2_scales[:])
+        banks = {i: finish_first_norm(i) for i in second}
 
-        residual_and_second_matmul(0)
-        for i in half_tiles(1):
+        for i in first:
+            add_b2(i)
+        quantise(nc, w2_grouped[:].rearrange("p c t -> p (c t)"), w2_codes[:], w2_scales[:])
+        for i in first:
+            second_matmul(i)
+        for i in second:
             round_h(i, banks[i])
-        g2_full = keep(nc.scalar.copy, "g2_full", spread(["g2"], "plain"))
-        s2_full = keep(nc.scalar.copy, "s2_full", spread(["s2"], "plain"))
+        add_b2(second[0])
         add_residual_and_relu(0)
-        residual_and_second_matmul(1)
-        for i in half_tiles(0):
+        for i in second[1:]:
+            add_b2(i)
+        for i in second:
+            second_matmul(i)
+        for i in first:
             sum_squared_deviations(nc, work, ln2, i)
-        standard_deviations(nc, ln2, 0, eps_col)
+        inverse_deviations(nc, ln2, 0, eps_col)
+        centre_and_gain(nc, work, ln2, first[0], g2_full)
         add_residual_and_relu(1)
-        for i in half_tiles(0):
+        for i in first[1:]:
             centre_and_gain(nc, work, ln2, i, g2_full)
         store_second_norm(0)
-        for i in half_tiles(1):
+        for i in second:
             centre_and_gain(nc, work, ln2, i, g2_full)
             sum_squared_deviations(nc, work, ln2, i)
-        standard_deviations(nc, ln2, 1, eps_col)
+        inverse_deviations(nc, ln2, 1, eps_col)
         store_second_norm(1)

@@ -19,8 +19,8 @@ TILES = N_TOKENS // P
 HALF = TILES // 2
 PASSES_1 = D_IN // K_PASS
 EPS = 1e-5
-X_AHEAD = 6
-MX_AHEAD = 3
+Q_AHEAD = 6
+MX_AHEAD = 4
 
 FLOPS = 2 * N_TOKENS * D_IN * D + 2 * N_TOKENS * D * D
 
@@ -190,7 +190,7 @@ def tile_multiscalegatencoder_pa_kernel(
             for s in range(PASSES_1 * 2):
                 nc.tensor.transpose(xt[:, s, :], x_words[:, s * P : (s + 1) * P], ident_f32[:])
             grouped = work.tile(
-                [P, PASSES_1 * P * PACK], BF16, align_bytes=64, tag="x_grouped", bufs=6
+                [P, PASSES_1 * P * PACK], BF16, align_bytes=64, tag="x_grouped", bufs=TILES
             )
             nc.scalar.copy(
                 out=grouped[:].bitcast(F32).rearrange("p (g r u) -> p g r u", g=PASSES_1, u=2),
@@ -199,8 +199,8 @@ def tile_multiscalegatencoder_pa_kernel(
             x_grouped[i] = grouped
 
         def quantise_x(i):
-            codes = work.tile([P, PASSES_1 * P], U32, align_bytes=64, tag="x_codes")
-            scales = work.tile([P, PASSES_1 * P], U8, align_bytes=64, tag="x_scales")
+            codes = work.tile([P, PASSES_1 * P], U32, align_bytes=64, tag="x_codes", bufs=TILES)
+            scales = work.tile([P, PASSES_1 * P], U8, align_bytes=64, tag="x_scales", bufs=TILES)
             quantise(nc, x_grouped[i][:], codes[:], scales[:])
             x_mx[i] = (codes, scales)
 
@@ -257,6 +257,7 @@ def tile_multiscalegatencoder_pa_kernel(
         b1_bank = spread(0)
         g1_bank = spread(1)
         s1_bank = spread(2)
+        b1_full = keep(nc.scalar.copy, "b1_full", b1_bank)
         transpose_x(0)
         for g in range(PASSES_1):
             w_grouped = work.tile([P, D, PACK], BF16, align_bytes=64, tag="w_grouped", bufs=2)
@@ -264,27 +265,22 @@ def tile_multiscalegatencoder_pa_kernel(
             quantise(
                 nc, w_grouped[:].rearrange("p c t -> p (c t)"), w1_codes[:, g, :], w1_scales[:, g, :]
             )
-        transpose_x(1)
-        transpose_x(2)
-        b1_full = keep(nc.scalar.copy, "b1_full", b1_bank)
-        for i in range(3, X_AHEAD):
-            transpose_x(i)
-        quantise_x(0)
-        first_matmul(0)
         g1_full = keep(nc.vector.tensor_copy, "g1_full", g1_bank)
-        quantise_x(1)
-        first_matmul(1)
         s1_full = keep(nc.vector.tensor_copy, "s1_full", s1_bank)
-        for i in range(2, MX_AHEAD):
+        for i in range(1, TILES - 1):
+            transpose_x(i)
+        for i in range(Q_AHEAD):
             quantise_x(i)
+        first_matmul(0)
+        transpose_x(TILES - 1)
+        for i in range(1, MX_AHEAD):
             first_matmul(i)
 
         for i in range(TILES):
             pre = add_to_bank(z1[i], b1_full)
-            if i + X_AHEAD < TILES:
-                transpose_x(i + X_AHEAD)
+            if i + Q_AHEAD < TILES:
+                quantise_x(i + Q_AHEAD)
             if i + MX_AHEAD < TILES:
-                quantise_x(i + MX_AHEAD)
                 first_matmul(i + MX_AHEAD)
             relu_and_sum(nc, work, ln1, i, pre)
             if i == HALF - 1:
@@ -320,10 +316,10 @@ def tile_multiscalegatencoder_pa_kernel(
         banks = {i: finish_first_norm(i) for i in first}
         for i in first:
             round_h(i, banks[i])
-        banks = {i: finish_first_norm(i) for i in second}
-
         for i in first:
             add_b2(i)
+        banks = {i: finish_first_norm(i) for i in second}
+
         quantise(nc, w2_grouped[:].rearrange("p c t -> p (c t)"), w2_codes[:], w2_scales[:])
         for i in first:
             second_matmul(i)

@@ -16,21 +16,14 @@ N_TOKENS = 1024
 D_IN = 1024
 D = 512
 TILES = N_TOKENS // P
-HALF = TILES // 2
 PASSES_1 = D_IN // K_PASS
 EPS = 1e-5
-Q_AHEAD = 6
-MX_AHEAD = 4
 
 FLOPS = 2 * N_TOKENS * D_IN * D + 2 * N_TOKENS * D * D
 
 
-def half_tiles(h):
-    return range(h * HALF, (h + 1) * HALF)
-
-
-def half_cols(h):
-    return slice(h * HALF, (h + 1) * HALF)
+def block(b):
+    return slice(b * P, (b + 1) * P)
 
 
 def regroup(copy, grouped, raw):
@@ -42,71 +35,6 @@ def regroup(copy, grouped, raw):
 
 def quantise(nc, grouped, codes, scales):
     nc.vector.quantize_mx(out=codes.bitcast(FP8X4), scales=scales, in_=grouped)
-
-
-def new_layer_norm(const, layer):
-    names = ["total", "neg_mean", "sq_dev", "rstd"]
-    ln = {n: const.tile([P, TILES], F32, name=n + layer) for n in names}
-    ln["act"] = {}
-    ln["centred"] = {}
-    return ln
-
-
-def relu_and_sum(nc, work, ln, i, pre):
-    act = work.tile([P, D], F32, tag="act", bufs=TILES)
-    nc.scalar.activation(
-        out=act[:], in_=pre[:], func=ACT.Relu, accum_out=ln["total"][:, i : i + 1]
-    )
-    ln["act"][i] = act
-
-
-def negate_means(nc, ln, h):
-    nc.scalar.mul(out=ln["neg_mean"][:, half_cols(h)], in_=ln["total"][:, half_cols(h)], mul=-1.0 / D)
-
-
-def sum_squared_deviations(nc, work, ln, i):
-    squares = work.tile([P, D], F32, tag="squares", bufs=2)
-    nc.scalar.activation(
-        out=squares[:],
-        in_=ln["act"][i][:],
-        func=ACT.Square,
-        bias=ln["neg_mean"][:, i : i + 1],
-        accum_out=ln["sq_dev"][:, i : i + 1],
-    )
-
-
-def inverse_deviations(nc, ln, h, eps_col):
-    nc.scalar.activation(
-        out=ln["rstd"][:, half_cols(h)],
-        in_=ln["sq_dev"][:, half_cols(h)],
-        func=ACT.Abs_reciprocal_sqrt,
-        bias=eps_col[:],
-        scale=1.0 / D,
-    )
-
-
-def centre_and_gain(nc, work, ln, i, gain):
-    centred = work.tile([P, D], F32, tag="centred", bufs=TILES)
-    nc.vector.scalar_tensor_tensor(
-        out=centred[:],
-        in0=ln["act"][i][:],
-        scalar=ln["neg_mean"][:, i : i + 1],
-        in1=gain[:],
-        op0=ALU.add,
-        op1=ALU.mult,
-    )
-    ln["centred"][i] = centred
-
-
-def scale_and_shift(nc, ln, i, shift, result):
-    nc.vector.scalar_tensor_tensor(
-        out=result[:],
-        in0=ln["centred"][i][:],
-        scalar=ln["rstd"][:, i : i + 1],
-        in1=shift[:],
-        op0=ALU.mult,
-        op1=ALU.add,
-    )
 
 
 def tile_multiscalegatencoder_pa_kernel(
@@ -136,19 +64,17 @@ def tile_multiscalegatencoder_pa_kernel(
 
         vec_rows = const.tile([P, D], BF16)
         nc.vector.memset(vec_rows[:], 0.0)
-
         load_w1(0)
-        for r, vec in enumerate([b1, ln1_g, ln1_b]):
+        for r, vec in enumerate([b1, ln1_g, ln1_b, b2]):
             nc.sync.dma_start(out=vec_rows[r : r + 1, :], in_=vec.unsqueeze(0))
         load_x(0)
         load_w1(1)
         for i in range(1, TILES):
             load_x(i)
         nc.sync.dma_start(out=w2_raw[:], in_=W2.rearrange("(t p) c -> p t c", p=P))
-        b2_full = const.tile([P, D], BF16)
         g2_full = const.tile([P, D], BF16)
         s2_full = const.tile([P, D], BF16)
-        for full, vec in [(b2_full, b2), (g2_full, ln2_g), (s2_full, ln2_b)]:
+        for full, vec in [(g2_full, ln2_g), (s2_full, ln2_b)]:
             nc.sync.dma_start(out=full[:], in_=vec.partition_broadcast(P))
 
         ident_bf16 = const.tile([P, P], BF16)
@@ -160,187 +86,242 @@ def tile_multiscalegatencoder_pa_kernel(
         warm = const.tile([P, 1], F32)
         nc.scalar.activation(out=warm[:], in_=eps_col[:], func=ACT.Abs_reciprocal_sqrt)
 
-        def spread(r):
-            bank = psum.tile([P, D], F32, tag="mx")
-            nc.tensor.matmul(
-                out=bank[:],
-                lhsT=ident_bf16[:, r : r + 1].to_broadcast([P, P]),
-                rhs=vec_rows[:],
-                start=True,
-                stop=True,
-            )
+        def spread(*rows):
+            bank = psum.tile([P, D], F32, tag="mx", bufs=4)
+            for r in rows:
+                nc.tensor.matmul(
+                    out=bank[:],
+                    lhsT=ident_bf16[:, r : r + 1].to_broadcast([P, P]),
+                    rhs=vec_rows[:],
+                    start=(r == rows[0]),
+                    stop=(r == rows[-1]),
+                )
             return bank
 
-        def keep(copy, name, bank):
-            full = const.tile([P, D], F32, name=name)
-            copy(out=full[:], in_=bank[:])
-            return full
-
-        x_grouped, x_mx, z1, z2, h1, h1_b2, h_grouped = {}, {}, {}, {}, {}, {}, {}
-        ln1 = new_layer_norm(const, "1")
-        ln2 = new_layer_norm(const, "2")
+        x_grouped, x_mx, z1, a1, tok, cen1, u1, ht, h_grouped = {}, {}, {}, {}, {}, {}, {}, {}, {}
+        z2, act2, cen2, h_mx, pre1, x_banks = {}, {}, {}, {}, {}, {}
         w1_codes = const.tile([P, PASSES_1, D], U32, align_bytes=64)
         w1_scales = const.tile([P, PASSES_1, D], U8, align_bytes=64)
         w2_codes = const.tile([P, D], U32, align_bytes=64)
         w2_scales = const.tile([P, D], U8, align_bytes=64)
+        neg_mean1 = const.tile([P, TILES], F32)
+        sq_dev1 = const.tile([P, TILES], F32)
+        rstd1 = const.tile([P, TILES], F32)
+        total2 = const.tile([P, TILES], F32)
+        neg_mean2 = const.tile([P, TILES], F32)
+        sq_dev2 = const.tile([P, TILES], F32)
+        rstd2 = const.tile([P, TILES], F32)
+        total1 = const.tile([P, TILES], F32)
 
-        def transpose_x(i):
+        def trans_x(i):
             x_words = x_sb[:, i, :].bitcast(F32)
-            xt = psum.tile([P, PASSES_1 * 2, P], F32, tag="plain")
+            xt = psum.tile([P, PASSES_1 * 2, P], F32, tag="mx" if i % 2 else "tp", bufs=4)
             for s in range(PASSES_1 * 2):
                 nc.tensor.transpose(xt[:, s, :], x_words[:, s * P : (s + 1) * P], ident_f32[:])
-            grouped = work.tile(
-                [P, PASSES_1 * P * PACK], BF16, align_bytes=64, tag="x_grouped", bufs=TILES
-            )
-            nc.scalar.copy(
-                out=grouped[:].bitcast(F32).rearrange("p (g r u) -> p g r u", g=PASSES_1, u=2),
-                in_=xt[:].rearrange("p (g u) r -> p g r u", u=2),
-            )
-            x_grouped[i] = grouped
+            x_banks[i] = xt
 
-        def quantise_x(i):
-            codes = work.tile([P, PASSES_1 * P], U32, align_bytes=64, tag="x_codes", bufs=TILES)
-            scales = work.tile([P, PASSES_1 * P], U8, align_bytes=64, tag="x_scales", bufs=TILES)
-            quantise(nc, x_grouped[i][:], codes[:], scales[:])
+        def copy_x(i):
+            x_grouped_tile = work.tile(
+                [P, PASSES_1, P, PACK], BF16, align_bytes=64, tag="x_grouped", bufs=TILES
+            )
+            x_grouped[i] = x_grouped_tile
+            nc.scalar.copy(
+                out=x_grouped[i][:].bitcast(F32),
+                in_=x_banks[i][:].rearrange("p (g u) r -> p g r u", u=2),
+            )
+
+        def quant_x(i):
+            codes = work.tile([P, PASSES_1, P], U32, align_bytes=64, tag="x_codes", bufs=TILES)
+            scales = work.tile([P, PASSES_1, P], U8, align_bytes=64, tag="x_scales", bufs=TILES)
+            quantise(
+                nc,
+                x_grouped[i][:].rearrange("p g r t -> p (g r t)"),
+                codes[:].rearrange("p g r -> p (g r)"),
+                scales[:].rearrange("p g r -> p (g r)"),
+            )
             x_mx[i] = (codes, scales)
 
-        def first_matmul(i):
-            x_codes, x_scales = x_mx[i]
-            bank = psum.tile([P, D], F32, tag="mx")
+        def mx1(i):
+            codes, scales = x_mx[i]
+            z1_tile = psum.tile([P, D], F32, tag="mx", bufs=4)
+            z1[i] = z1_tile
             for g in range(PASSES_1):
-                tokens = slice(g * P, (g + 1) * P)
                 nc.tensor.matmul_mx(
-                    out=bank[:],
-                    lhsT=x_codes[:, tokens].bitcast(FP8X4),
-                    lhsT_scale=x_scales[:, tokens],
+                    out=z1[i][:],
+                    lhsT=codes[:, g, :].bitcast(FP8X4),
+                    lhsT_scale=scales[:, g, :],
                     rhs=w1_codes[:, g, :].bitcast(FP8X4),
                     rhs_scale=w1_scales[:, g, :],
                     start=(g == 0),
                     stop=(g == PASSES_1 - 1),
                 )
-            z1[i] = bank
 
-        def add_to_bank(bank, addend):
-            pre = work.tile([P, D], F32, tag="pre", bufs=5)
-            nc.vector.tensor_tensor(out=pre[:], in0=bank[:], in1=addend[:], op=ALU.add)
-            return pre
+        def bias1(i):
+            pre1_tile = work.tile([P, D], F32, tag="pre1", bufs=TILES)
+            pre1[i] = pre1_tile
+            nc.vector.tensor_tensor(out=pre1[i][:], in0=z1[i][:], in1=b1_full[:], op=ALU.add)
 
-        def finish_first_norm(i):
-            h1[i] = work.tile([P, D], F32, name="h1", bufs=TILES)
-            scale_and_shift(nc, ln1, i, s1_full, h1[i])
-            ht = psum.tile([P, PACK, P], F32, tag="plain")
-            for t in range(PACK):
-                nc.tensor.transpose(ht[:, t, :], h1[i][:, t * P : (t + 1) * P], ident_f32[:])
-            return ht
+        def relu1(i):
+            a1_tile = work.tile([P, D], F32, tag="a1", bufs=TILES)
+            tok[i] = a1_tile
+            nc.scalar.activation(out=tok[i][:], in_=pre1[i][:], func=ACT.Relu, accum_out=total1[:, i : i + 1])
+            nc.scalar.mul(out=neg_mean1[:, i : i + 1], in_=total1[:, i : i + 1], mul=-1.0 / D)
 
-        def round_h(i, ht):
-            grouped = work.tile([P, P, PACK], BF16, align_bytes=64, tag="h_grouped", bufs=TILES)
-            nc.scalar.copy(out=grouped[:], in_=ht[:].rearrange("p t r -> p r t"))
-            h_grouped[i] = grouped
+        def centre1(i):
+            cen1_tile = work.tile([P, D], F32, tag="cen1", bufs=TILES)
+            cen1[i] = cen1_tile
+            nc.vector.scalar_tensor_tensor(
+                out=cen1[i][:],
+                in0=tok[i][:],
+                scalar=neg_mean1[:, i : i + 1],
+                in1=g1_full[:],
+                op0=ALU.add,
+                op1=ALU.mult,
+            )
 
-        def second_matmul(i):
-            h_codes = work.tile([P, P], U32, align_bytes=64, bufs=5)
-            h_scales = work.tile([P, P], U8, align_bytes=64, bufs=5)
-            quantise(nc, h_grouped[i][:].rearrange("p r t -> p (r t)"), h_codes[:], h_scales[:])
-            bank = psum.tile([P, D], F32, tag="mx")
+        def square1(i):
+            squares = work.tile([P, D], F32, tag="squares", bufs=2)
+            nc.scalar.activation(
+                out=squares[:], in_=tok[i][:], func=ACT.Square,
+                bias=neg_mean1[:, i : i + 1], accum_out=sq_dev1[:, i : i + 1],
+            )
+            nc.scalar.activation(
+                out=rstd1[:, i : i + 1], in_=sq_dev1[:, i : i + 1],
+                func=ACT.Abs_reciprocal_sqrt, bias=eps_col[:], scale=1.0 / D,
+            )
+
+        def scale1(i):
+            u1_tile = work.tile([P, D], F32, tag="u1", bufs=TILES)
+            u1[i] = u1_tile
+            nc.vector.scalar_tensor_tensor(
+                out=u1[i][:], in0=cen1[i][:], scalar=rstd1[:, i : i + 1], in1=s1_b2_full[:],
+                op0=ALU.mult, op1=ALU.add,
+            )
+
+        def trans_h(i):
+            ht_tile = psum.tile([P, PACK, P], F32, tag="tp", bufs=4)
+            ht[i] = ht_tile
+            for n, addend in enumerate((minus_b2_full, u1[i])):
+                for t in range(PACK):
+                    nc.tensor.matmul(
+                        out=ht[i][:, t, :],
+                        lhsT=addend[:, block(t)],
+                        rhs=ident_f32[:],
+                        is_transpose=True,
+                        start=(n == 0 and t == 0),
+                        stop=(n == 1 and t == PACK - 1),
+                    )
+
+        def round_h(i):
+            h_grouped_tile = work.tile([P, P, PACK], BF16, align_bytes=64, tag="h_grouped", bufs=TILES)
+            h_grouped[i] = h_grouped_tile
+            nc.scalar.copy(out=h_grouped[i][:], in_=ht[i][:].rearrange("p t r -> p r t"))
+
+        def quant_h(i):
+            codes = work.tile([P, P], U32, align_bytes=64, tag="h_codes", bufs=TILES)
+            scales = work.tile([P, P], U8, align_bytes=64, tag="h_scales", bufs=TILES)
+            quantise(nc, h_grouped[i][:].rearrange("p r t -> p (r t)"), codes[:], scales[:])
+            h_mx[i] = (codes, scales)
+
+        def second(i):
+            codes, scales = h_mx[i]
+            z2_tile = psum.tile([P, D], F32, tag="mx", bufs=4)
+            z2[i] = z2_tile
             nc.tensor.matmul_mx(
-                out=bank[:],
-                lhsT=h_codes[:].bitcast(FP8X4),
-                lhsT_scale=h_scales[:],
+                out=z2[i][:],
+                lhsT=codes[:].bitcast(FP8X4),
+                lhsT_scale=scales[:],
                 rhs=w2_codes[:].bitcast(FP8X4),
                 rhs_scale=w2_scales[:],
                 start=True,
                 stop=True,
             )
-            z2[i] = bank
+
+        def residual(i):
+            act2_tile = work.tile([P, D], F32, tag="pre2", bufs=TILES)
+            act2[i] = act2_tile
+            nc.vector.tensor_tensor(out=act2[i][:], in0=z2[i][:], in1=u1[i][:], op=ALU.add)
+
+        def relu2(i):
+            act = work.tile([P, D], F32, tag="act2", bufs=TILES)
+            nc.scalar.activation(out=act[:], in_=act2[i][:], func=ACT.Relu, accum_out=total2[:, i : i + 1])
+            act2[i] = act
+            nc.scalar.mul(out=neg_mean2[:, i : i + 1], in_=total2[:, i : i + 1], mul=-1.0 / D)
+
+        def centre2(i):
+            cen2_tile = work.tile([P, D], F32, tag="cen2", bufs=TILES)
+            cen2[i] = cen2_tile
+            nc.vector.scalar_tensor_tensor(
+                out=cen2[i][:], in0=act2[i][:], scalar=neg_mean2[:, i : i + 1], in1=g2_full[:],
+                op0=ALU.add, op1=ALU.mult,
+            )
+
+        def square2(i):
+            squares = work.tile([P, D], F32, tag="squares", bufs=2)
+            nc.scalar.activation(
+                out=squares[:], in_=act2[i][:], func=ACT.Square,
+                bias=neg_mean2[:, i : i + 1], accum_out=sq_dev2[:, i : i + 1],
+            )
+            nc.scalar.activation(
+                out=rstd2[:, i : i + 1], in_=sq_dev2[:, i : i + 1],
+                func=ACT.Abs_reciprocal_sqrt, bias=eps_col[:], scale=1.0 / D,
+            )
+
+        def scale2(i):
+            result = work.tile([P, D], F32)
+            nc.vector.scalar_tensor_tensor(
+                out=result[:], in0=cen2[i][:], scalar=rstd2[:, i : i + 1], in1=s2_full[:],
+                op0=ALU.mult, op1=ALU.add,
+            )
+            nc.sync.dma_start(out=out[i * P : (i + 1) * P, :], in_=result[:])
 
         b1_bank = spread(0)
+        b1_full = const.tile([P, D], F32)
+        nc.scalar.copy(out=b1_full[:], in_=b1_bank[:])
         g1_bank = spread(1)
-        s1_bank = spread(2)
-        b1_full = keep(nc.scalar.copy, "b1_full", b1_bank)
-        transpose_x(0)
+        s1_b2_bank = spread(2, 3)
+        minus_b2_bank = spread(3)
+        g1_full = const.tile([P, D], F32)
+        nc.scalar.copy(out=g1_full[:], in_=g1_bank[:])
         for g in range(PASSES_1):
             w_grouped = work.tile([P, D, PACK], BF16, align_bytes=64, tag="w_grouped", bufs=2)
             regroup(nc.vector.tensor_copy, w_grouped, w1_raw[:, g])
-            quantise(
-                nc, w_grouped[:].rearrange("p c t -> p (c t)"), w1_codes[:, g, :], w1_scales[:, g, :]
-            )
-        g1_full = keep(nc.vector.tensor_copy, "g1_full", g1_bank)
-        s1_full = keep(nc.vector.tensor_copy, "s1_full", s1_bank)
-        for i in range(1, TILES - 1):
-            transpose_x(i)
-        for i in range(Q_AHEAD):
-            quantise_x(i)
-        first_matmul(0)
-        transpose_x(TILES - 1)
-        for i in range(1, MX_AHEAD):
-            first_matmul(i)
+            quantise(nc, w_grouped[:].rearrange("p c t -> p (c t)"), w1_codes[:, g, :], w1_scales[:, g, :])
+        s1_b2_full = const.tile([P, D], F32)
+        nc.scalar.copy(out=s1_b2_full[:], in_=s1_b2_bank[:])
+        minus_b2_full = const.tile([P, D], F32)
+        nc.scalar.mul(out=minus_b2_full[:], in_=minus_b2_bank[:], mul=-1.0)
 
-        for i in range(TILES):
-            pre = add_to_bank(z1[i], b1_full)
-            if i + Q_AHEAD < TILES:
-                quantise_x(i + Q_AHEAD)
-            if i + MX_AHEAD < TILES:
-                first_matmul(i + MX_AHEAD)
-            relu_and_sum(nc, work, ln1, i, pre)
-            if i == HALF - 1:
-                negate_means(nc, ln1, 0)
-        negate_means(nc, ln1, 1)
+        def pipeline(stages):
+            for step in range(TILES + max(lag for lag, stage in stages)):
+                for lag, stage in stages:
+                    if 0 <= step - lag < TILES:
+                        stage(step - lag)
 
-        for h in range(2):
-            for i in half_tiles(h):
-                centre_and_gain(nc, work, ln1, i, g1_full)
-                sum_squared_deviations(nc, work, ln1, i)
-            inverse_deviations(nc, ln1, h, eps_col)
-
+        pipeline([
+            (0, trans_x),
+            (1, copy_x),
+            (3, quant_x),
+            (3, mx1),
+            (5, bias1),
+            (5, relu1),
+        ])
         w2_grouped = work.tile([P, D, PACK], BF16, align_bytes=64, tag="w_grouped", bufs=2)
-        regroup(nc.scalar.copy, w2_grouped, w2_raw[:])
-
-        def add_b2(i):
-            h1_b2[i] = work.tile([P, D], F32, name="h1_b2", bufs=TILES)
-            nc.vector.tensor_tensor(out=h1_b2[i][:], in0=h1[i][:], in1=b2_full[:], op=ALU.add)
-
-        def add_residual_and_relu(h):
-            for i in half_tiles(h):
-                pre2 = add_to_bank(z2[i], h1_b2[i])
-                relu_and_sum(nc, work, ln2, i, pre2)
-            negate_means(nc, ln2, h)
-
-        def store_second_norm(h):
-            for i in half_tiles(h):
-                result = work.tile([P, D], F32)
-                scale_and_shift(nc, ln2, i, s2_full, result)
-                nc.sync.dma_start(out=out[i * P : (i + 1) * P, :], in_=result[:])
-
-        first, second = list(half_tiles(0)), list(half_tiles(1))
-        banks = {i: finish_first_norm(i) for i in first}
-        for i in first:
-            round_h(i, banks[i])
-        for i in first:
-            add_b2(i)
-        banks = {i: finish_first_norm(i) for i in second}
-
+        regroup(nc.vector.tensor_copy, w2_grouped, w2_raw[:])
         quantise(nc, w2_grouped[:].rearrange("p c t -> p (c t)"), w2_codes[:], w2_scales[:])
-        for i in first:
-            second_matmul(i)
-        for i in second:
-            round_h(i, banks[i])
-        add_b2(second[0])
-        add_residual_and_relu(0)
-        for i in second[1:]:
-            add_b2(i)
-        for i in second:
-            second_matmul(i)
-        for i in first:
-            sum_squared_deviations(nc, work, ln2, i)
-        inverse_deviations(nc, ln2, 0, eps_col)
-        centre_and_gain(nc, work, ln2, first[0], g2_full)
-        add_residual_and_relu(1)
-        for i in first[1:]:
-            centre_and_gain(nc, work, ln2, i, g2_full)
-        store_second_norm(0)
-        for i in second:
-            centre_and_gain(nc, work, ln2, i, g2_full)
-            sum_squared_deviations(nc, work, ln2, i)
-        inverse_deviations(nc, ln2, 1, eps_col)
-        store_second_norm(1)
+        pipeline([
+            (0, centre1),
+            (0, square1),
+            (2, scale1),
+            (2, trans_h),
+            (3, round_h),
+            (5, quant_h),
+            (5, second),
+            (8, residual),
+        ])
+        pipeline([
+            (0, relu2),
+            (1, centre2),
+            (2, square2),
+            (3, scale2),
+        ])

@@ -16,6 +16,7 @@ N_TOKENS = 1024
 D_IN = 1024
 D = 512
 TILES = N_TOKENS // P
+BLOCKS = D // P
 PASSES_1 = D_IN // K_PASS
 EPS = 1e-5
 
@@ -62,19 +63,24 @@ def tile_multiscalegatencoder_pa_kernel(
                 ),
             )
 
-        vec_rows = const.tile([P, D], BF16)
-        nc.vector.memset(vec_rows[:], 0.0)
+        b1_row = const.tile([P, D], BF16)
+        nc.vector.memset(b1_row[:], 0.0)
+        b2_rows = const.tile([P, P], BF16)
+        nc.vector.memset(b2_rows[:], 0.0)
         load_w1(0)
-        for r, vec in enumerate([b1, ln1_g, ln1_b, b2]):
-            nc.sync.dma_start(out=vec_rows[r : r + 1, :], in_=vec.unsqueeze(0))
+        nc.sync.dma_start(out=b1_row[0:1, :], in_=b1.unsqueeze(0))
+        nc.sync.dma_start(out=b2_rows[0:BLOCKS, :], in_=b2.rearrange("(t p) -> t p", p=P))
         load_x(0)
         load_w1(1)
         for i in range(1, TILES):
             load_x(i)
         nc.sync.dma_start(out=w2_raw[:], in_=W2.rearrange("(t p) c -> p t c", p=P))
+        g1_full = const.tile([P, D], BF16)
+        s1_full = const.tile([P, D], BF16)
+        b2_full = const.tile([P, D], BF16)
         g2_full = const.tile([P, D], BF16)
         s2_full = const.tile([P, D], BF16)
-        for full, vec in [(g2_full, ln2_g), (s2_full, ln2_b)]:
+        for full, vec in [(g1_full, ln1_g), (s1_full, ln1_b), (b2_full, b2), (g2_full, ln2_g), (s2_full, ln2_b)]:
             nc.sync.dma_start(out=full[:], in_=vec.partition_broadcast(P))
 
         ident_bf16 = const.tile([P, P], BF16)
@@ -86,19 +92,13 @@ def tile_multiscalegatencoder_pa_kernel(
         warm = const.tile([P, 1], F32)
         nc.scalar.activation(out=warm[:], in_=eps_col[:], func=ACT.Abs_reciprocal_sqrt)
 
-        def spread(*rows):
-            bank = psum.tile([P, D], F32, tag="mx", bufs=4)
-            for r in rows:
-                nc.tensor.matmul(
-                    out=bank[:],
-                    lhsT=ident_bf16[:, r : r + 1].to_broadcast([P, P]),
-                    rhs=vec_rows[:],
-                    start=(r == rows[0]),
-                    stop=(r == rows[-1]),
-                )
-            return bank
+        minus_blocks = const.tile([P, BLOCKS, P], BF16)
+        nc.gpsimd.tensor_scalar(
+            out=minus_blocks[:], in0=ident_bf16[:, 0:BLOCKS].unsqueeze(2).to_broadcast([P, BLOCKS, P]),
+            scalar1=-1.0, scalar2=0.0, op0=ALU.mult, op1=ALU.add,
+        )
 
-        x_grouped, x_mx, z1, a1, tok, cen1, u1, ht, h_grouped = {}, {}, {}, {}, {}, {}, {}, {}, {}
+        x_grouped, x_mx, z1, tok, cen1, u1, ht, h_grouped = {}, {}, {}, {}, {}, {}, {}, {}
         z2, act2, cen2, h_mx, pre1, x_banks = {}, {}, {}, {}, {}, {}
         w1_codes = const.tile([P, PASSES_1, D], U32, align_bytes=64)
         w1_scales = const.tile([P, PASSES_1, D], U8, align_bytes=64)
@@ -165,7 +165,12 @@ def tile_multiscalegatencoder_pa_kernel(
             a1_tile = work.tile([P, D], F32, tag="a1", bufs=TILES)
             tok[i] = a1_tile
             nc.scalar.activation(out=tok[i][:], in_=pre1[i][:], func=ACT.Relu, accum_out=total1[:, i : i + 1])
-            nc.scalar.mul(out=neg_mean1[:, i : i + 1], in_=total1[:, i : i + 1], mul=-1.0 / D)
+
+        def mean1(i):
+            if i % 2:
+                nc.gpsimd.tensor_scalar(
+                    out=neg_mean1[:, i - 1 : i + 1], in0=total1[:, i - 1 : i + 1], scalar1=-1.0 / D, scalar2=0.0, op0=ALU.mult, op1=ALU.add
+                )
 
         def centre1(i):
             cen1_tile = work.tile([P, D], F32, tag="cen1", bufs=TILES)
@@ -185,10 +190,13 @@ def tile_multiscalegatencoder_pa_kernel(
                 out=squares[:], in_=tok[i][:], func=ACT.Square,
                 bias=neg_mean1[:, i : i + 1], accum_out=sq_dev1[:, i : i + 1],
             )
-            nc.scalar.activation(
-                out=rstd1[:, i : i + 1], in_=sq_dev1[:, i : i + 1],
-                func=ACT.Abs_reciprocal_sqrt, bias=eps_col[:], scale=1.0 / D,
-            )
+
+        def inv1(i):
+            if i % 2:
+                nc.scalar.activation(
+                    out=rstd1[:, i - 1 : i + 1], in_=sq_dev1[:, i - 1 : i + 1],
+                    func=ACT.Abs_reciprocal_sqrt, bias=eps_col[:], scale=1.0 / D,
+                )
 
         def scale1(i):
             u1_tile = work.tile([P, D], F32, tag="u1", bufs=TILES)
@@ -201,16 +209,15 @@ def tile_multiscalegatencoder_pa_kernel(
         def trans_h(i):
             ht_tile = psum.tile([P, PACK, P], F32, tag="tp", bufs=4)
             ht[i] = ht_tile
-            for n, addend in enumerate((minus_b2_full, u1[i])):
-                for t in range(PACK):
-                    nc.tensor.matmul(
-                        out=ht[i][:, t, :],
-                        lhsT=addend[:, block(t)],
-                        rhs=ident_f32[:],
-                        is_transpose=True,
-                        start=(n == 0 and t == 0),
-                        stop=(n == 1 and t == PACK - 1),
-                    )
+            nc.tensor.matmul(
+                out=ht[i][:].rearrange("p t r -> p (t r)"), lhsT=b2_rows[:],
+                rhs=minus_blocks[:].rearrange("k t r -> k (t r)"), start=True, stop=False,
+            )
+            for t in range(PACK):
+                nc.tensor.matmul(
+                    out=ht[i][:, t, :], lhsT=u1[i][:, block(t)], rhs=ident_f32[:],
+                    is_transpose=True, start=False, stop=(t == PACK - 1),
+                )
 
         def round_h(i):
             h_grouped_tile = work.tile([P, P, PACK], BF16, align_bytes=64, tag="h_grouped", bufs=TILES)
@@ -246,7 +253,12 @@ def tile_multiscalegatencoder_pa_kernel(
             act = work.tile([P, D], F32, tag="act2", bufs=TILES)
             nc.scalar.activation(out=act[:], in_=act2[i][:], func=ACT.Relu, accum_out=total2[:, i : i + 1])
             act2[i] = act
-            nc.scalar.mul(out=neg_mean2[:, i : i + 1], in_=total2[:, i : i + 1], mul=-1.0 / D)
+
+        def mean2(i):
+            if i % 2:
+                nc.gpsimd.tensor_scalar(
+                    out=neg_mean2[:, i - 1 : i + 1], in0=total2[:, i - 1 : i + 1], scalar1=-1.0 / D, scalar2=0.0, op0=ALU.mult, op1=ALU.add
+                )
 
         def centre2(i):
             cen2_tile = work.tile([P, D], F32, tag="cen2", bufs=TILES)
@@ -262,35 +274,32 @@ def tile_multiscalegatencoder_pa_kernel(
                 out=squares[:], in_=act2[i][:], func=ACT.Square,
                 bias=neg_mean2[:, i : i + 1], accum_out=sq_dev2[:, i : i + 1],
             )
-            nc.scalar.activation(
-                out=rstd2[:, i : i + 1], in_=sq_dev2[:, i : i + 1],
-                func=ACT.Abs_reciprocal_sqrt, bias=eps_col[:], scale=1.0 / D,
-            )
+
+        def inv2(i):
+            if i % 2:
+                nc.scalar.activation(
+                    out=rstd2[:, i - 1 : i + 1], in_=sq_dev2[:, i - 1 : i + 1],
+                    func=ACT.Abs_reciprocal_sqrt, bias=eps_col[:], scale=1.0 / D,
+                )
 
         def scale2(i):
-            result = work.tile([P, D], F32)
+            result = work.tile([P, D], F32, tag="result", bufs=TILES)
             nc.vector.scalar_tensor_tensor(
                 out=result[:], in0=cen2[i][:], scalar=rstd2[:, i : i + 1], in1=s2_full[:],
                 op0=ALU.mult, op1=ALU.add,
             )
             nc.sync.dma_start(out=out[i * P : (i + 1) * P, :], in_=result[:])
 
-        b1_bank = spread(0)
+        b1_bank = psum.tile([P, D], F32, tag="mx", bufs=4)
+        nc.tensor.matmul(
+            out=b1_bank[:], lhsT=ident_bf16[:, 0:1].to_broadcast([P, P]), rhs=b1_row[:], start=True, stop=True
+        )
         b1_full = const.tile([P, D], F32)
         nc.scalar.copy(out=b1_full[:], in_=b1_bank[:])
-        g1_bank = spread(1)
-        s1_b2_bank = spread(2, 3)
-        minus_b2_bank = spread(3)
-        g1_full = const.tile([P, D], F32)
-        nc.scalar.copy(out=g1_full[:], in_=g1_bank[:])
         for g in range(PASSES_1):
             w_grouped = work.tile([P, D, PACK], BF16, align_bytes=64, tag="w_grouped", bufs=2)
             regroup(nc.vector.tensor_copy, w_grouped, w1_raw[:, g])
             quantise(nc, w_grouped[:].rearrange("p c t -> p (c t)"), w1_codes[:, g, :], w1_scales[:, g, :])
-        s1_b2_full = const.tile([P, D], F32)
-        nc.scalar.copy(out=s1_b2_full[:], in_=s1_b2_bank[:])
-        minus_b2_full = const.tile([P, D], F32)
-        nc.scalar.mul(out=minus_b2_full[:], in_=minus_b2_bank[:], mul=-1.0)
 
         def pipeline(stages):
             for step in range(TILES + max(lag for lag, stage in stages)):
@@ -305,23 +314,29 @@ def tile_multiscalegatencoder_pa_kernel(
             (3, mx1),
             (5, bias1),
             (5, relu1),
+            (6, mean1),
         ])
+        s1_b2_full = const.tile([P, D], F32)
+        nc.vector.tensor_tensor(out=s1_b2_full[:], in0=s1_full[:], in1=b2_full[:], op=ALU.add)
         w2_grouped = work.tile([P, D, PACK], BF16, align_bytes=64, tag="w_grouped", bufs=2)
         regroup(nc.vector.tensor_copy, w2_grouped, w2_raw[:])
         quantise(nc, w2_grouped[:].rearrange("p c t -> p (c t)"), w2_codes[:], w2_scales[:])
         pipeline([
             (0, centre1),
             (0, square1),
-            (2, scale1),
-            (2, trans_h),
-            (3, round_h),
-            (5, quant_h),
-            (5, second),
-            (8, residual),
+            (1, inv1),
+            (3, scale1),
+            (3, trans_h),
+            (4, round_h),
+            (7, quant_h),
+            (7, second),
+            (10, residual),
         ])
         pipeline([
             (0, relu2),
-            (1, centre2),
+            (1, mean2),
             (2, square2),
-            (3, scale2),
+            (3, centre2),
+            (3, inv2),
+            (6, scale2),
         ])

@@ -168,9 +168,7 @@ def tile_multiscalegatencoder_pa_kernel(
 
         def mean1(i):
             if i % 2:
-                nc.gpsimd.tensor_scalar(
-                    out=neg_mean1[:, i - 1 : i + 1], in0=total1[:, i - 1 : i + 1], scalar1=-1.0 / D, scalar2=0.0, op0=ALU.mult, op1=ALU.add
-                )
+                nc.scalar.mul(out=neg_mean1[:, i - 1 : i + 1], in_=total1[:, i - 1 : i + 1], mul=-1.0 / D)
 
         def centre1(i):
             cen1_tile = work.tile([P, D], F32, tag="cen1", bufs=TILES)
@@ -256,9 +254,7 @@ def tile_multiscalegatencoder_pa_kernel(
 
         def mean2(i):
             if i % 2:
-                nc.gpsimd.tensor_scalar(
-                    out=neg_mean2[:, i - 1 : i + 1], in0=total2[:, i - 1 : i + 1], scalar1=-1.0 / D, scalar2=0.0, op0=ALU.mult, op1=ALU.add
-                )
+                nc.scalar.mul(out=neg_mean2[:, i - 1 : i + 1], in_=total2[:, i - 1 : i + 1], mul=-1.0 / D)
 
         def centre2(i):
             cen2_tile = work.tile([P, D], F32, tag="cen2", bufs=TILES)
@@ -301,11 +297,30 @@ def tile_multiscalegatencoder_pa_kernel(
             regroup(nc.vector.tensor_copy, w_grouped, w1_raw[:, g])
             quantise(nc, w_grouped[:].rearrange("p c t -> p (c t)"), w1_codes[:, g, :], w1_scales[:, g, :])
 
-        def pipeline(stages):
-            for step in range(TILES + max(lag for lag, stage in stages)):
+        s1_b2_full = const.tile([P, D], F32)
+        w2_grouped = work.tile([P, D, PACK], BF16, align_bytes=64, tag="w_grouped", bufs=2)
+
+        def sum_shift(i):
+            if i == 0:
+                nc.vector.tensor_tensor(out=s1_b2_full[:], in0=s1_full[:], in1=b2_full[:], op=ALU.add)
+
+        def w2_regroup(i):
+            if i < 4:
+                cols = slice(i * D // 4, (i + 1) * D // 4)
+                nc.scalar.copy(
+                    out=w2_grouped[:, cols, :].rearrange("p (c i) t -> p c t i", i=4),
+                    in_=w2_raw[:, :, cols].rearrange("p t (c i) -> p c t i", i=4),
+                )
+
+        def w2_quant(i):
+            if i == 0:
+                quantise(nc, w2_grouped[:].rearrange("p c t -> p (c t)"), w2_codes[:], w2_scales[:])
+
+        def pipeline(stages, tiles=range(TILES)):
+            for step in range(len(tiles) + max(lag for lag, stage in stages)):
                 for lag, stage in stages:
-                    if 0 <= step - lag < TILES:
-                        stage(step - lag)
+                    if 0 <= step - lag < len(tiles):
+                        stage(tiles[step - lag])
 
         pipeline([
             (0, trans_x),
@@ -316,27 +331,25 @@ def tile_multiscalegatencoder_pa_kernel(
             (5, relu1),
             (6, mean1),
         ])
-        s1_b2_full = const.tile([P, D], F32)
-        nc.vector.tensor_tensor(out=s1_b2_full[:], in0=s1_full[:], in1=b2_full[:], op=ALU.add)
-        w2_grouped = work.tile([P, D, PACK], BF16, align_bytes=64, tag="w_grouped", bufs=2)
-        regroup(nc.vector.tensor_copy, w2_grouped, w2_raw[:])
-        quantise(nc, w2_grouped[:].rearrange("p c t -> p (c t)"), w2_codes[:], w2_scales[:])
         pipeline([
             (0, centre1),
             (0, square1),
             (1, inv1),
+            (2, sum_shift),
+            (3, w2_regroup),
             (3, scale1),
             (3, trans_h),
-            (4, round_h),
-            (7, quant_h),
-            (7, second),
-            (10, residual),
+            (5, round_h),
+            (7, w2_quant),
+            (8, quant_h),
+            (8, second),
+            (11, residual),
         ])
         pipeline([
             (0, relu2),
             (1, mean2),
-            (2, square2),
+            (3, square2),
             (3, centre2),
-            (3, inv2),
+            (4, inv2),
             (6, scale2),
         ])

@@ -113,9 +113,22 @@ def tile_multiscalegatencoder_pa_kernel(
         rstd2 = const.tile([P, TILES], F32)
         total1 = const.tile([P, TILES], F32)
 
+        def keep_warm(bank):
+            nc.tensor.matmul_mx(
+                out=bank,
+                lhsT=w1_codes[:, 0, block(0)].bitcast(FP8X4),
+                lhsT_scale=w1_scales[:, 0, block(0)],
+                rhs=w1_codes[:, 0, :].bitcast(FP8X4),
+                rhs_scale=w1_scales[:, 0, :],
+                start=True,
+                stop=True,
+            )
+
         def trans_x(i):
             x_words = x_sb[:, i, :].bitcast(F32)
             xt = psum.tile([P, PASSES_1 * 2, P], F32, tag="mx" if i % 2 else "tp", bufs=4)
+            if i in (1, 2):
+                keep_warm(xt[:].rearrange("p s r -> p (s r)"))
             for s in range(PASSES_1 * 2):
                 nc.tensor.transpose(xt[:, s, :], x_words[:, s * P : (s + 1) * P], ident_f32[:])
             x_banks[i] = xt
@@ -292,6 +305,9 @@ def tile_multiscalegatencoder_pa_kernel(
         )
         b1_full = const.tile([P, D], F32)
         nc.scalar.copy(out=b1_full[:], in_=b1_bank[:])
+        idle_bank = psum.tile([P, D], F32, tag="tp", bufs=4)
+        for n in range(2):
+            nc.tensor.matmul(out=idle_bank[:, block(n)], lhsT=ident_f32[:], rhs=ident_f32[:], start=True, stop=True)
         for g in range(PASSES_1):
             w_grouped = work.tile([P, D, PACK], BF16, align_bytes=64, tag="w_grouped", bufs=2)
             regroup(nc.vector.tensor_copy, w_grouped, w1_raw[:, g])

@@ -332,40 +332,34 @@ def tile_multiscalegatencoder_pa_kernel(
             if i == 0:
                 quantise(nc, w2_grouped[:].rearrange("p c t -> p (c t)"), w2_codes[:], w2_scales[:])
 
-        def pipeline(stages, tiles=range(TILES)):
-            for step in range(len(tiles) + max(lag for lag, stage in stages)):
-                for lag, stage in stages:
-                    if 0 <= step - lag < len(tiles):
-                        stage(tiles[step - lag])
-
-        pipeline([
+        stages = [
+            (20, second),
             (0, trans_x),
-            (1, copy_x),
-            (3, quant_x),
             (3, mx1),
-            (5, bias1),
-            (5, relu1),
+            (14, trans_h),
+            (22, residual),
+            (12, scale1),
+            (3, bias1),
+            (17, quant_h),
+            (1, quant_x),
+            (17, w2_quant),
             (6, mean1),
-        ])
-        pipeline([
-            (0, centre1),
-            (0, square1),
-            (1, inv1),
-            (2, sum_shift),
-            (3, w2_regroup),
-            (3, scale1),
-            (3, trans_h),
-            (5, round_h),
-            (7, w2_quant),
-            (8, quant_h),
-            (8, second),
-            (11, residual),
-        ])
-        pipeline([
-            (0, relu2),
-            (1, mean2),
-            (3, square2),
-            (3, centre2),
-            (4, inv2),
-            (6, scale2),
-        ])
+            (5, relu1),
+            (23, mean2),
+            (22, relu2),
+            (15, round_h),
+            (0, copy_x),
+            (12, w2_regroup),
+            (8, centre1),
+            (28, centre2),
+            (30, scale2),
+            (10, sum_shift),
+            (9, inv1),
+            (7, square1),
+            (25, inv2),
+            (24, square2),
+        ]
+        for step in range(TILES + max(lag for lag, stage in stages)):
+            for lag, stage in stages:
+                if 0 <= step - lag < TILES:
+                    stage(step - lag)

@@ -52,8 +52,10 @@ def tile_multiscalegatencoder_pa_kernel(
         w1_raw = const.tile([P, PASSES_1, PACK, D], BF16)
         w2_raw = const.tile([P, PACK, D], BF16)
 
-        def load_x(i):
-            nc.sync.dma_start(out=x_sb[:, i, :], in_=x[i * P : (i + 1) * P, :])
+        def load_x(first, count):
+            j, e = first // 2, first % 2
+            pair = x[2 * j * P : (2 * j + 2) * P, :].rearrange("(p e) k -> p e k", e=2)
+            nc.sync.dma_start(out=x_sb[:, first : first + count, :], in_=pair[:, e : e + count, :])
 
         def load_w1(g):
             nc.sync.dma_start(
@@ -70,10 +72,11 @@ def tile_multiscalegatencoder_pa_kernel(
         load_w1(0)
         nc.sync.dma_start(out=b1_row[0:1, :], in_=b1.unsqueeze(0))
         nc.sync.dma_start(out=b2_rows[0:BLOCKS, :], in_=b2.rearrange("(t p) -> t p", p=P))
-        load_x(0)
+        load_x(0, 1)
         load_w1(1)
-        for i in range(1, TILES):
-            load_x(i)
+        load_x(1, 1)
+        for i in range(2, TILES, 2):
+            load_x(i, 2)
         nc.sync.dma_start(out=w2_raw[:], in_=W2.rearrange("(t p) c -> p t c", p=P))
         g1_full = const.tile([P, D], BF16)
         s1_full = const.tile([P, D], BF16)
@@ -297,7 +300,9 @@ def tile_multiscalegatencoder_pa_kernel(
                 out=result[:], in0=cen2[i][:], scalar=rstd2[:, i : i + 1], in1=s2_full[:],
                 op0=ALU.mult, op1=ALU.add,
             )
-            nc.sync.dma_start(out=out[i * P : (i + 1) * P, :], in_=result[:])
+            j, e = i // 2, i % 2
+            pair = out[2 * j * P : (2 * j + 2) * P, :].rearrange("(p e) c -> p e c", e=2)
+            nc.sync.dma_start(out=pair[:, e, :], in_=result[:])
 
         b1_bank = psum.tile([P, D], F32, tag="mx", bufs=4)
         nc.tensor.matmul(

@@ -296,13 +296,16 @@ def tile_multiscalegatencoder_pa_kernel(
 
         def scale2(i):
             result = work.tile([P, D], F32, tag="result", bufs=TILES)
-            nc.vector.scalar_tensor_tensor(
-                out=result[:], in0=cen2[i][:], scalar=rstd2[:, i : i + 1], in1=s2_full[:],
-                op0=ALU.mult, op1=ALU.add,
-            )
             j, e = i // 2, i % 2
             pair = out[2 * j * P : (2 * j + 2) * P, :].rearrange("(p e) c -> p e c", e=2)
-            nc.sync.dma_start(out=pair[:, e, :], in_=result[:])
+            pieces = 2 if i == TILES - 1 else 1
+            for n in range(pieces):
+                cols = slice(n * D // pieces, (n + 1) * D // pieces)
+                nc.vector.scalar_tensor_tensor(
+                    out=result[:, cols], in0=cen2[i][:, cols], scalar=rstd2[:, i : i + 1], in1=s2_full[:, cols],
+                    op0=ALU.mult, op1=ALU.add,
+                )
+                nc.sync.dma_start(out=pair[:, e, cols], in_=result[:, cols])
 
         b1_bank = psum.tile([P, D], F32, tag="mx", bufs=4)
         nc.tensor.matmul(

@@ -128,6 +128,8 @@ def tile_multiscalegatencoder_pa_kernel(
             )
 
         def trans_x(i):
+            if i in x_banks:
+                return
             x_words = x_sb[:, i, :].bitcast(F32)
             xt = psum.tile([P, PASSES_1 * 2, P], F32, tag="mx" if i % 2 else "tp", bufs=4)
             if i in (1, 2):
@@ -137,6 +139,8 @@ def tile_multiscalegatencoder_pa_kernel(
             x_banks[i] = xt
 
         def copy_x(i):
+            if i in x_grouped:
+                return
             x_grouped_tile = work.tile(
                 [P, PASSES_1, P, PACK], BF16, align_bytes=64, tag="x_grouped", bufs=TILES
             )
@@ -147,6 +151,8 @@ def tile_multiscalegatencoder_pa_kernel(
             )
 
         def quant_x(i):
+            if i in x_mx:
+                return
             codes = work.tile([P, PASSES_1, P], U32, align_bytes=64, tag="x_codes", bufs=TILES)
             scales = work.tile([P, PASSES_1, P], U8, align_bytes=64, tag="x_scales", bufs=TILES)
             quantise(
@@ -316,13 +322,26 @@ def tile_multiscalegatencoder_pa_kernel(
         idle_bank = psum.tile([P, D], F32, tag="tp", bufs=4)
         for n in range(2):
             nc.tensor.matmul(out=idle_bank[:, block(n)], lhsT=ident_f32[:], rhs=ident_f32[:], start=True, stop=True)
-        for g in range(PASSES_1):
-            w_grouped = work.tile([P, D, PACK], BF16, align_bytes=64, tag="w_grouped", bufs=2)
+        w1_grouped = {}
+
+        def w1_regroup(g):
+            w_grouped = work.tile([P, D, PACK], BF16, align_bytes=64, tag="w_grouped", bufs=3)
+            w1_grouped[g] = w_grouped
             regroup(nc.vector.tensor_copy, w_grouped, w1_raw[:, g])
-            quantise(nc, w_grouped[:].rearrange("p c t -> p (c t)"), w1_codes[:, g, :], w1_scales[:, g, :])
+
+        def w1_quant(g):
+            quantise(nc, w1_grouped[g][:].rearrange("p c t -> p (c t)"), w1_codes[:, g, :], w1_scales[:, g, :])
+
+        w1_regroup(0)
+        w1_quant(0)
+        w1_regroup(1)
+        trans_x(0)
+        copy_x(0)
+        quant_x(0)
+        w1_quant(1)
 
         s1_b2_full = const.tile([P, D], F32)
-        w2_grouped = work.tile([P, D, PACK], BF16, align_bytes=64, tag="w_grouped", bufs=2)
+        w2_grouped = work.tile([P, D, PACK], BF16, align_bytes=64, tag="w_grouped", bufs=3)
 
         def sum_shift(i):
             if i == 0:

@@ -67,23 +67,22 @@ def tile_multiscalegatencoder_pa_kernel(
 
         b1_row = const.tile([P, D], BF16)
         nc.vector.memset(b1_row[:], 0.0)
-        b2_rows = const.tile([P, P], BF16)
-        nc.vector.memset(b2_rows[:], 0.0)
+        shift_rows = const.tile([P, P], BF16)
+        nc.vector.memset(shift_rows[:], 0.0)
         load_w1(0)
         nc.sync.dma_start(out=b1_row[0:1, :], in_=b1.unsqueeze(0))
-        nc.sync.dma_start(out=b2_rows[0:BLOCKS, :], in_=b2.rearrange("(t p) -> t p", p=P))
+        nc.sync.dma_start(out=shift_rows[0:BLOCKS, :], in_=b2.rearrange("(t p) -> t p", p=P))
         load_x(0, 1)
         load_w1(1)
         load_x(1, 1)
         for i in range(2, TILES, 2):
             load_x(i, 2)
         nc.sync.dma_start(out=w2_raw[:], in_=W2.rearrange("(t p) c -> p t c", p=P))
+        nc.sync.dma_start(out=shift_rows[BLOCKS : 2 * BLOCKS, :], in_=ln1_b.rearrange("(t p) -> t p", p=P))
         g1_full = const.tile([P, D], BF16)
-        s1_full = const.tile([P, D], BF16)
-        b2_full = const.tile([P, D], BF16)
         g2_full = const.tile([P, D], BF16)
         s2_full = const.tile([P, D], BF16)
-        for full, vec in [(g1_full, ln1_g), (s1_full, ln1_b), (b2_full, b2), (g2_full, ln2_g), (s2_full, ln2_b)]:
+        for full, vec in [(g1_full, ln1_g), (g2_full, ln2_g), (s2_full, ln2_b)]:
             nc.sync.dma_start(out=full[:], in_=vec.partition_broadcast(P))
 
         ident_bf16 = const.tile([P, P], BF16)
@@ -131,7 +130,7 @@ def tile_multiscalegatencoder_pa_kernel(
             if i in x_banks:
                 return
             x_words = x_sb[:, i, :].bitcast(F32)
-            xt = psum.tile([P, PASSES_1 * 2, P], F32, tag="mx" if i % 2 else "tp", bufs=4)
+            xt = psum.tile([P, PASSES_1 * 2, P], F32, tag="mx" if i % 2 else "tp", bufs=3 if i % 2 else 4)
             if i in (1, 2):
                 keep_warm(xt[:].rearrange("p s r -> p (s r)"))
             for s in range(PASSES_1 * 2):
@@ -165,7 +164,7 @@ def tile_multiscalegatencoder_pa_kernel(
 
         def mx1(i):
             codes, scales = x_mx[i]
-            z1_tile = psum.tile([P, D], F32, tag="mx", bufs=4)
+            z1_tile = psum.tile([P, D], F32, tag="mx", bufs=3)
             z1[i] = z1_tile
             for g in range(PASSES_1):
                 nc.tensor.matmul_mx(
@@ -222,7 +221,7 @@ def tile_multiscalegatencoder_pa_kernel(
             u1_tile = work.tile([P, D], F32, tag="u1", bufs=TILES)
             u1[i] = u1_tile
             nc.vector.scalar_tensor_tensor(
-                out=u1[i][:], in0=cen1[i][:], scalar=rstd1[:, i : i + 1], in1=s1_b2_full[:],
+                out=u1[i][:], in0=cen1[i][:], scalar=rstd1[:, i : i + 1], in1=s1_b2_bank[:],
                 op0=ALU.mult, op1=ALU.add,
             )
 
@@ -230,7 +229,7 @@ def tile_multiscalegatencoder_pa_kernel(
             ht_tile = psum.tile([P, PACK, P], F32, tag="tp", bufs=4)
             ht[i] = ht_tile
             nc.tensor.matmul(
-                out=ht[i][:].rearrange("p t r -> p (t r)"), lhsT=b2_rows[:],
+                out=ht[i][:].rearrange("p t r -> p (t r)"), lhsT=shift_rows[:],
                 rhs=minus_blocks[:].rearrange("k t r -> k (t r)"), start=True, stop=False,
             )
             for t in range(PACK):
@@ -252,7 +251,7 @@ def tile_multiscalegatencoder_pa_kernel(
 
         def second(i):
             codes, scales = h_mx[i]
-            z2_tile = psum.tile([P, D], F32, tag="mx", bufs=4)
+            z2_tile = psum.tile([P, D], F32, tag="mx", bufs=3)
             z2[i] = z2_tile
             nc.tensor.matmul_mx(
                 out=z2[i][:],
@@ -313,7 +312,7 @@ def tile_multiscalegatencoder_pa_kernel(
                 )
                 nc.sync.dma_start(out=pair[:, e, cols], in_=result[:, cols])
 
-        b1_bank = psum.tile([P, D], F32, tag="mx", bufs=4)
+        b1_bank = psum.tile([P, D], F32, tag="mx", bufs=3)
         nc.tensor.matmul(
             out=b1_bank[:], lhsT=ident_bf16[:, 0:1].to_broadcast([P, P]), rhs=b1_row[:], start=True, stop=True
         )
@@ -340,12 +339,25 @@ def tile_multiscalegatencoder_pa_kernel(
         quant_x(0)
         w1_quant(1)
 
-        s1_b2_full = const.tile([P, D], F32)
+        s1_b2_bank = psum.tile([P, D], F32, tag="shift", bufs=1)
         w2_grouped = work.tile([P, D, PACK], BF16, align_bytes=64, tag="w_grouped", bufs=3)
+
+        shift_cols = const.tile([P, 2 * BLOCKS], F32)
+        sum_cols = const.tile([P, BLOCKS], F32)
 
         def sum_shift(i):
             if i == 0:
-                nc.vector.tensor_tensor(out=s1_b2_full[:], in0=s1_full[:], in1=b2_full[:], op=ALU.add)
+                turned = psum.tile([P, P], BF16, tag="tp", bufs=4)
+                nc.tensor.transpose(turned[:], shift_rows[:], ident_bf16[:])
+                nc.scalar.copy(out=shift_cols[:], in_=turned[:, 0 : 2 * BLOCKS])
+                nc.gpsimd.tensor_tensor(
+                    out=sum_cols[:], in0=shift_cols[:, 0:BLOCKS], in1=shift_cols[:, BLOCKS : 2 * BLOCKS], op=ALU.add
+                )
+            if i == 1:
+                for t in range(BLOCKS):
+                    nc.tensor.transpose(
+                        s1_b2_bank[:, block(t)], sum_cols[:, t : t + 1].to_broadcast([P, P]), ident_f32[:]
+                    )
 
         def w2_regroup(i):
             if i < 4:

@@ -29,7 +29,7 @@ def block(b):
 
 def regroup(copy, grouped, raw):
     copy(
-        out=grouped[:].rearrange("p (c i) t -> p c t i", i=4),
+        out=grouped.rearrange("p (c i) t -> p c t i", i=4),
         in_=raw.rearrange("p t (c i) -> p c t i", i=4),
     )
 
@@ -323,16 +323,23 @@ def tile_multiscalegatencoder_pa_kernel(
             nc.tensor.matmul(out=idle_bank[:, block(n)], lhsT=ident_f32[:], rhs=ident_f32[:], start=True, stop=True)
         w1_grouped = {}
 
-        def w1_regroup(g):
+        for g in range(PASSES_1):
             w_grouped = work.tile([P, D, PACK], BF16, align_bytes=64, tag="w_grouped", bufs=3)
             w1_grouped[g] = w_grouped
-            regroup(nc.vector.tensor_copy, w_grouped, w1_raw[:, g])
 
-        def w1_quant(g):
-            quantise(nc, w1_grouped[g][:].rearrange("p c t -> p (c t)"), w1_codes[:, g, :], w1_scales[:, g, :])
+        def w1_regroup(g, cols=slice(0, D)):
+            regroup(nc.vector.tensor_copy, w1_grouped[g][:, cols, :], w1_raw[:, g, :, cols])
 
-        w1_regroup(0)
-        w1_quant(0)
+        def w1_quant(g, cols=slice(0, D)):
+            quantise(
+                nc, w1_grouped[g][:, cols, :].rearrange("p c t -> p (c t)"), w1_codes[:, g, cols], w1_scales[:, g, cols]
+            )
+
+        halves = (slice(0, D // 2), slice(D // 2, D))
+        for cols in halves:
+            w1_regroup(0, cols)
+        for cols in halves:
+            w1_quant(0, cols)
         w1_regroup(1)
         trans_x(0)
         copy_x(0)

@@ -19,6 +19,7 @@ TILES = N_TOKENS // P
 BLOCKS = D // P
 PASSES_1 = D_IN // K_PASS
 EPS = 1e-5
+ON_POOL = (0,)
 
 FLOPS = 2 * N_TOKENS * D_IN * D + 2 * N_TOKENS * D * D
 
@@ -78,7 +79,10 @@ def tile_multiscalegatencoder_pa_kernel(
         for i in range(2, TILES, 2):
             load_x(i, 2)
         nc.sync.dma_start(out=w2_raw[:], in_=W2.rearrange("(t p) c -> p t c", p=P))
-        nc.sync.dma_start(out=shift_rows[BLOCKS : 2 * BLOCKS, :], in_=ln1_b.rearrange("(t p) -> t p", p=P))
+        for n, vec in enumerate([ln1_b, ln2_g, ln2_b]):
+            nc.sync.dma_start(
+                out=shift_rows[(n + 1) * BLOCKS : (n + 2) * BLOCKS, :], in_=vec.rearrange("(t p) -> t p", p=P)
+            )
         g1_full = const.tile([P, D], BF16)
         g2_full = const.tile([P, D], BF16)
         s2_full = const.tile([P, D], BF16)
@@ -280,8 +284,10 @@ def tile_multiscalegatencoder_pa_kernel(
         def centre2(i):
             cen2_tile = work.tile([P, D], F32, tag="cen2", bufs=TILES)
             cen2[i] = cen2_tile
+            if i in ON_POOL:
+                return
             nc.vector.scalar_tensor_tensor(
-                out=cen2[i][:], in0=act2[i][:], scalar=neg_mean2[:, i : i + 1], in1=g2_full[:],
+                out=cen2[i][:], in0=act2[i][:], scalar=neg_mean2[:, i : i + 1], in1=affine2[0][:, 0, :],
                 op0=ALU.add, op1=ALU.mult,
             )
 
@@ -299,15 +305,31 @@ def tile_multiscalegatencoder_pa_kernel(
                     func=ACT.Abs_reciprocal_sqrt, bias=eps_col[:], scale=1.0 / D,
                 )
 
+        pool_results = {}
+
+        def store_pool(i):
+            if i in ON_POOL:
+                nc.sync.dma_start(out=pool_results[i][0], in_=pool_results[i][1][:])
+
         def scale2(i):
             result = work.tile([P, D], F32, tag="result", bufs=TILES)
             j, e = i // 2, i % 2
             pair = out[2 * j * P : (2 * j + 2) * P, :].rearrange("(p e) c -> p e c", e=2)
+            if i in ON_POOL:
+                gained = work.tile([P, D], F32, tag="gained2", bufs=3)
+                nc.gpsimd.tensor_scalar(
+                    out=cen2[i][:], in0=act2[i][:], scalar1=neg_mean2[:, i : i + 1],
+                    scalar2=rstd2[:, i : i + 1], op0=ALU.add, op1=ALU.mult,
+                )
+                nc.gpsimd.tensor_tensor(out=gained[:], in0=cen2[i][:], in1=g2_full[:], op=ALU.mult)
+                nc.gpsimd.tensor_tensor(out=result[:], in0=gained[:], in1=s2_full[:], op=ALU.add)
+                pool_results[i] = (pair[:, e, :], result)
+                return
             pieces = 2 if i == TILES - 1 else 1
             for n in range(pieces):
                 cols = slice(n * D // pieces, (n + 1) * D // pieces)
                 nc.vector.scalar_tensor_tensor(
-                    out=result[:, cols], in0=cen2[i][:, cols], scalar=rstd2[:, i : i + 1], in1=s2_full[:, cols],
+                    out=result[:, cols], in0=cen2[i][:, cols], scalar=rstd2[:, i : i + 1], in1=affine2[0][:, 1, cols],
                     op0=ALU.mult, op1=ALU.add,
                 )
                 nc.sync.dma_start(out=pair[:, e, cols], in_=result[:, cols])
@@ -346,7 +368,9 @@ def tile_multiscalegatencoder_pa_kernel(
         quant_x(0)
         w1_quant(1)
 
-        s1_b2_bank = psum.tile([P, D], F32, tag="shift", bufs=1)
+        s1_b2_bank = psum.tile([P, D], F32, tag="affine", bufs=1)
+        affine2 = {}
+        affine_cols = const.tile([P, 2 * BLOCKS], BF16)
         w2_grouped = work.tile([P, D, PACK], BF16, align_bytes=64, tag="w_grouped", bufs=3)
 
         shift_cols = const.tile([P, 2 * BLOCKS], F32)
@@ -357,6 +381,7 @@ def tile_multiscalegatencoder_pa_kernel(
                 turned = psum.tile([P, P], BF16, tag="tp", bufs=4)
                 nc.tensor.transpose(turned[:], shift_rows[:], ident_bf16[:])
                 nc.scalar.copy(out=shift_cols[:], in_=turned[:, 0 : 2 * BLOCKS])
+                nc.scalar.copy(out=affine_cols[:], in_=turned[:, 2 * BLOCKS : 4 * BLOCKS])
                 nc.gpsimd.tensor_tensor(
                     out=sum_cols[:], in0=shift_cols[:, 0:BLOCKS], in1=shift_cols[:, BLOCKS : 2 * BLOCKS], op=ALU.add
                 )
@@ -364,6 +389,16 @@ def tile_multiscalegatencoder_pa_kernel(
                 for t in range(BLOCKS):
                     nc.tensor.transpose(
                         s1_b2_bank[:, block(t)], sum_cols[:, t : t + 1].to_broadcast([P, P]), ident_f32[:]
+                    )
+
+        def spread2(i):
+            if i == TILES - 1:
+                bank = psum.tile([P, 2, D], BF16, tag="affine", bufs=1)
+                affine2[0] = bank
+                for t in range(2 * BLOCKS):
+                    nc.tensor.transpose(
+                        bank[:, t // BLOCKS, block(t % BLOCKS)],
+                        affine_cols[:, t : t + 1].to_broadcast([P, P]), ident_bf16[:],
                     )
 
         def w2_regroup(i):
@@ -380,6 +415,8 @@ def tile_multiscalegatencoder_pa_kernel(
 
         stages = [
             (20, second),
+            (20, spread2),
+            (33, store_pool),
             (0, trans_x),
             (3, mx1),
             (14, trans_h),

@@ -78,15 +78,16 @@ def tile_multiscalegatencoder_pa_kernel(
         load_x(1, 1)
         for i in range(2, TILES, 2):
             load_x(i, 2)
-        nc.sync.dma_start(out=w2_raw[:], in_=W2.rearrange("(t p) c -> p t c", p=P))
+        g1_full = const.tile([P, D], BF16)
+        nc.sync.dma_start(out=g1_full[:], in_=ln1_g.partition_broadcast(P))
         for n, vec in enumerate([ln1_b, ln2_g, ln2_b]):
             nc.sync.dma_start(
                 out=shift_rows[(n + 1) * BLOCKS : (n + 2) * BLOCKS, :], in_=vec.rearrange("(t p) -> t p", p=P)
             )
-        g1_full = const.tile([P, D], BF16)
+        nc.sync.dma_start(out=w2_raw[:], in_=W2.rearrange("(t p) c -> p t c", p=P))
         g2_full = const.tile([P, D], BF16)
         s2_full = const.tile([P, D], BF16)
-        for full, vec in [(g1_full, ln1_g), (g2_full, ln2_g), (s2_full, ln2_b)]:
+        for full, vec in [(g2_full, ln2_g), (s2_full, ln2_b)]:
             nc.sync.dma_start(out=full[:], in_=vec.partition_broadcast(P))
 
         ident_bf16 = const.tile([P, P], BF16)

@@ -278,9 +278,15 @@ def tile_multiscalegatencoder_pa_kernel(
             nc.scalar.activation(out=act[:], in_=act2[i][:], func=ACT.Relu, accum_out=total2[:, i : i + 1])
             act2[i] = act
 
+        def stat_cols(i):
+            if i >= TILES - 2:
+                return slice(i, i + 1)
+            return slice(i - 1, i + 1) if i % 2 else None
+
         def mean2(i):
-            if i % 2:
-                nc.scalar.mul(out=neg_mean2[:, i - 1 : i + 1], in_=total2[:, i - 1 : i + 1], mul=-1.0 / D)
+            cols = stat_cols(i)
+            if cols:
+                nc.scalar.mul(out=neg_mean2[:, cols], in_=total2[:, cols], mul=-1.0 / D)
 
         def centre2(i):
             cen2_tile = work.tile([P, D], F32, tag="cen2", bufs=TILES)
@@ -300,9 +306,10 @@ def tile_multiscalegatencoder_pa_kernel(
             )
 
         def inv2(i):
-            if i % 2:
+            cols = stat_cols(i)
+            if cols:
                 nc.scalar.activation(
-                    out=rstd2[:, i - 1 : i + 1], in_=sq_dev2[:, i - 1 : i + 1],
+                    out=rstd2[:, cols], in_=sq_dev2[:, cols],
                     func=ACT.Abs_reciprocal_sqrt, bias=eps_col[:], scale=1.0 / D,
                 )
 
@@ -415,13 +422,13 @@ def tile_multiscalegatencoder_pa_kernel(
                 quantise(nc, w2_grouped[:].rearrange("p c t -> p (c t)"), w2_codes[:], w2_scales[:])
 
         stages = [
-            (20, second),
-            (20, spread2),
-            (33, store_pool),
+            (19, second),
+            (19, spread2),
+            (31, store_pool),
             (0, trans_x),
             (3, mx1),
             (14, trans_h),
-            (22, residual),
+            (21, residual),
             (12, scale1),
             (3, bias1),
             (17, quant_h),
@@ -429,19 +436,19 @@ def tile_multiscalegatencoder_pa_kernel(
             (17, w2_quant),
             (6, mean1),
             (5, relu1),
-            (23, mean2),
-            (22, relu2),
+            (22, mean2),
+            (21, relu2),
             (15, round_h),
             (0, copy_x),
             (12, w2_regroup),
             (8, centre1),
-            (28, centre2),
-            (30, scale2),
+            (26, centre2),
+            (28, scale2),
             (10, sum_shift),
             (9, inv1),
             (7, square1),
-            (25, inv2),
-            (24, square2),
+            (24, inv2),
+            (23, square2),
         ]
         for step in range(TILES + max(lag for lag, stage in stages)):
             for lag, stage in stages:

@@ -422,13 +422,13 @@ def tile_multiscalegatencoder_pa_kernel(
                 quantise(nc, w2_grouped[:].rearrange("p c t -> p (c t)"), w2_codes[:], w2_scales[:])
 
         stages = [
-            (19, second),
-            (19, spread2),
-            (31, store_pool),
+            (20, second),
+            (20, spread2),
+            (32, store_pool),
             (0, trans_x),
             (3, mx1),
             (14, trans_h),
-            (21, residual),
+            (22, residual),
             (12, scale1),
             (3, bias1),
             (17, quant_h),
@@ -436,19 +436,19 @@ def tile_multiscalegatencoder_pa_kernel(
             (17, w2_quant),
             (6, mean1),
             (5, relu1),
-            (22, mean2),
-            (21, relu2),
+            (24, mean2),
+            (23, relu2),
             (15, round_h),
             (0, copy_x),
             (12, w2_regroup),
             (8, centre1),
-            (26, centre2),
-            (28, scale2),
+            (27, centre2),
+            (29, scale2),
             (10, sum_shift),
             (9, inv1),
             (7, square1),
-            (24, inv2),
-            (23, square2),
+            (26, inv2),
+            (25, square2),
         ]
         for step in range(TILES + max(lag for lag, stage in stages)):
             for lag, stage in stages:

@@ -19,7 +19,8 @@ TILES = N_TOKENS // P
 BLOCKS = D // P
 PASSES_1 = D_IN // K_PASS
 EPS = 1e-5
-ON_POOL = (0,)
+SUM_ON_VECTOR = (4,)
+POOL_FROM = {0: 0, 1: 256}
 
 FLOPS = 2 * N_TOKENS * D_IN * D + 2 * N_TOKENS * D * D
 
@@ -275,7 +276,13 @@ def tile_multiscalegatencoder_pa_kernel(
 
         def relu2(i):
             act = work.tile([P, D], F32, tag="act2", bufs=TILES)
-            nc.scalar.activation(out=act[:], in_=act2[i][:], func=ACT.Relu, accum_out=total2[:, i : i + 1])
+            if i in SUM_ON_VECTOR:
+                nc.vector.tensor_scalar(
+                    out=act[:], in0=act2[i][:], scalar1=0.0, scalar2=None, op0=ALU.max, op1=ALU.add,
+                    accum_out=total2[:, i : i + 1],
+                )
+            else:
+                nc.scalar.activation(out=act[:], in_=act2[i][:], func=ACT.Relu, accum_out=total2[:, i : i + 1])
             act2[i] = act
 
         def stat_cols(i):
@@ -291,12 +298,12 @@ def tile_multiscalegatencoder_pa_kernel(
         def centre2(i):
             cen2_tile = work.tile([P, D], F32, tag="cen2", bufs=TILES)
             cen2[i] = cen2_tile
-            if i in ON_POOL:
-                return
-            nc.vector.scalar_tensor_tensor(
-                out=cen2[i][:], in0=act2[i][:], scalar=neg_mean2[:, i : i + 1], in1=affine2[0][:, 0, :],
-                op0=ALU.add, op1=ALU.mult,
-            )
+            cols = slice(0, POOL_FROM.get(i, D))
+            if cols.stop:
+                nc.vector.scalar_tensor_tensor(
+                    out=cen2[i][:, cols], in0=act2[i][:, cols], scalar=neg_mean2[:, i : i + 1],
+                    in1=affine2[0][:, 0, cols], op0=ALU.add, op1=ALU.mult,
+                )
 
         def square2(i):
             squares = work.tile([P, D], F32, tag="squares", bufs=2)
@@ -316,26 +323,29 @@ def tile_multiscalegatencoder_pa_kernel(
         pool_results = {}
 
         def store_pool(i):
-            if i in ON_POOL:
-                nc.sync.dma_start(out=pool_results[i][0], in_=pool_results[i][1][:])
+            if i in POOL_FROM:
+                nc.sync.dma_start(out=pool_results[i][0], in_=pool_results[i][1])
 
         def scale2(i):
             result = work.tile([P, D], F32, tag="result", bufs=TILES)
             j, e = i // 2, i % 2
             pair = out[2 * j * P : (2 * j + 2) * P, :].rearrange("(p e) c -> p e c", e=2)
-            if i in ON_POOL:
+            width = POOL_FROM.get(i, D)
+            if width < D:
+                cols = slice(width, D)
                 gained = work.tile([P, D], F32, tag="gained2", bufs=3)
                 nc.gpsimd.tensor_scalar(
-                    out=cen2[i][:], in0=act2[i][:], scalar1=neg_mean2[:, i : i + 1],
+                    out=cen2[i][:, cols], in0=act2[i][:, cols], scalar1=neg_mean2[:, i : i + 1],
                     scalar2=rstd2[:, i : i + 1], op0=ALU.add, op1=ALU.mult,
                 )
-                nc.gpsimd.tensor_tensor(out=gained[:], in0=cen2[i][:], in1=g2_full[:], op=ALU.mult)
-                nc.gpsimd.tensor_tensor(out=result[:], in0=gained[:], in1=s2_full[:], op=ALU.add)
-                pool_results[i] = (pair[:, e, :], result)
+                nc.gpsimd.tensor_tensor(out=gained[:, cols], in0=cen2[i][:, cols], in1=g2_full[:, cols], op=ALU.mult)
+                nc.gpsimd.tensor_tensor(out=result[:, cols], in0=gained[:, cols], in1=s2_full[:, cols], op=ALU.add)
+                pool_results[i] = (pair[:, e, cols], result[:, cols])
+            if width == 0:
                 return
             pieces = 2 if i == TILES - 1 else 1
             for n in range(pieces):
-                cols = slice(n * D // pieces, (n + 1) * D // pieces)
+                cols = slice(n * width // pieces, (n + 1) * width // pieces)
                 nc.vector.scalar_tensor_tensor(
                     out=result[:, cols], in0=cen2[i][:, cols], scalar=rstd2[:, i : i + 1], in1=affine2[0][:, 1, cols],
                     op0=ALU.mult, op1=ALU.add,
@@ -424,7 +434,7 @@ def tile_multiscalegatencoder_pa_kernel(
         stages = [
             (20, second),
             (20, spread2),
-            (32, store_pool),
+            (33, store_pool),
             (0, trans_x),
             (3, mx1),
             (14, trans_h),

@@ -19,7 +19,7 @@ TILES = N_TOKENS // P
 BLOCKS = D // P
 PASSES_1 = D_IN // K_PASS
 EPS = 1e-5
-SUM_ON_VECTOR = (4,)
+SUM_ON_VECTOR = (3,)
 POOL_FROM = {0: 0, 1: 256}
 
 FLOPS = 2 * N_TOKENS * D_IN * D + 2 * N_TOKENS * D * D

import concourse.mybir as mybir
from concourse.masks import make_identity

F32 = mybir.dt.float32
BF16 = mybir.dt.bfloat16
U32 = mybir.dt.uint32
U8 = mybir.dt.uint8
FP8X4 = mybir.dt.float8_e4m3fn_x4
ALU = mybir.AluOpType
ACT = mybir.ActivationFunctionType

P = 128
PACK = 4
K_PASS = P * PACK
N_TOKENS = 1024
D_IN = 1024
D = 512
TILES = N_TOKENS // P
BLOCKS = D // P
PASSES_1 = D_IN // K_PASS
EPS = 1e-5
SUM_ON_VECTOR = (3,)
POOL_FROM = {0: 0, 1: 256}

FLOPS = 2 * N_TOKENS * D_IN * D + 2 * N_TOKENS * D * D


def block(b):
    return slice(b * P, (b + 1) * P)


def regroup(copy, grouped, raw):
    copy(
        out=grouped.rearrange("p (c i) t -> p c t i", i=4),
        in_=raw.rearrange("p t (c i) -> p c t i", i=4),
    )


def quantise(nc, grouped, codes, scales):
    nc.vector.quantize_mx(out=codes.bitcast(FP8X4), scales=scales, in_=grouped)


def tile_multiscalegatencoder_pa_kernel(
    tc, x, W1, b1, ln1_g, ln1_b, W2, b2, ln2_g, ln2_b, out
):
    nc = tc.nc
    with (
        tc.tile_pool(name="const", bufs=1) as const,
        tc.tile_pool(name="work", bufs=4) as work,
        tc.psum_pool(name="psum", bufs=4) as psum,
        tc.manual_schedule(),
    ):
        x_sb = const.tile([P, TILES, D_IN], BF16)
        w1_raw = const.tile([P, PASSES_1, PACK, D], BF16)
        w2_raw = const.tile([P, PACK, D], BF16)

        def load_x(first, count):
            j, e = first // 2, first % 2
            pair = x[2 * j * P : (2 * j + 2) * P, :].rearrange("(p e) k -> p e k", e=2)
            nc.sync.dma_start(out=x_sb[:, first : first + count, :], in_=pair[:, e : e + count, :])

        def load_w1(g):
            nc.sync.dma_start(
                out=w1_raw[:, g].rearrange("q (u e) c -> q u e c", u=2),
                in_=W1[g * K_PASS : (g + 1) * K_PASS, :].rearrange(
                    "(u q e) c -> q u e c", u=2, e=2
                ),
            )

        b1_row = const.tile([P, D], BF16)
        nc.vector.memset(b1_row[:], 0.0)
        shift_rows = const.tile([P, P], BF16)
        nc.vector.memset(shift_rows[:], 0.0)
        load_w1(0)
        nc.sync.dma_start(out=b1_row[0:1, :], in_=b1.unsqueeze(0))
        nc.sync.dma_start(out=shift_rows[0:BLOCKS, :], in_=b2.rearrange("(t p) -> t p", p=P))
        load_x(0, 1)
        load_w1(1)
        load_x(1, 1)
        for i in range(2, TILES, 2):
            load_x(i, 2)
        g1_full = const.tile([P, D], BF16)
        nc.sync.dma_start(out=g1_full[:], in_=ln1_g.partition_broadcast(P))
        for n, vec in enumerate([ln1_b, ln2_g, ln2_b]):
            nc.sync.dma_start(
                out=shift_rows[(n + 1) * BLOCKS : (n + 2) * BLOCKS, :], in_=vec.rearrange("(t p) -> t p", p=P)
            )
        nc.sync.dma_start(out=w2_raw[:], in_=W2.rearrange("(t p) c -> p t c", p=P))
        g2_full = const.tile([P, D], BF16)
        s2_full = const.tile([P, D], BF16)
        for full, vec in [(g2_full, ln2_g), (s2_full, ln2_b)]:
            nc.sync.dma_start(out=full[:], in_=vec.partition_broadcast(P))

        ident_bf16 = const.tile([P, P], BF16)
        make_identity(nc, ident_bf16[:])
        ident_f32 = const.tile([P, P], F32)
        make_identity(nc, ident_f32[:])
        eps_col = const.tile([P, 1], F32)
        nc.vector.memset(eps_col[:], EPS)
        warm = const.tile([P, 1], F32)
        nc.scalar.activation(out=warm[:], in_=eps_col[:], func=ACT.Abs_reciprocal_sqrt)

        minus_blocks = const.tile([P, BLOCKS, P], BF16)
        nc.gpsimd.tensor_scalar(
            out=minus_blocks[:], in0=ident_bf16[:, 0:BLOCKS].unsqueeze(2).to_broadcast([P, BLOCKS, P]),
            scalar1=-1.0, scalar2=0.0, op0=ALU.mult, op1=ALU.add,
        )

        x_grouped, x_mx, z1, tok, cen1, u1, ht, h_grouped = {}, {}, {}, {}, {}, {}, {}, {}
        z2, act2, cen2, h_mx, pre1, x_banks = {}, {}, {}, {}, {}, {}
        w1_codes = const.tile([P, PASSES_1, D], U32, align_bytes=64)
        w1_scales = const.tile([P, PASSES_1, D], U8, align_bytes=64)
        w2_codes = const.tile([P, D], U32, align_bytes=64)
        w2_scales = const.tile([P, D], U8, align_bytes=64)
        neg_mean1 = const.tile([P, TILES], F32)
        sq_dev1 = const.tile([P, TILES], F32)
        rstd1 = const.tile([P, TILES], F32)
        total2 = const.tile([P, TILES], F32)
        neg_mean2 = const.tile([P, TILES], F32)
        sq_dev2 = const.tile([P, TILES], F32)
        rstd2 = const.tile([P, TILES], F32)
        total1 = const.tile([P, TILES], F32)

        def keep_warm(bank):
            nc.tensor.matmul_mx(
                out=bank,
                lhsT=w1_codes[:, 0, block(0)].bitcast(FP8X4),
                lhsT_scale=w1_scales[:, 0, block(0)],
                rhs=w1_codes[:, 0, :].bitcast(FP8X4),
                rhs_scale=w1_scales[:, 0, :],
                start=True,
                stop=True,
            )

        def trans_x(i):
            if i in x_banks:
                return
            x_words = x_sb[:, i, :].bitcast(F32)
            xt = psum.tile([P, PASSES_1 * 2, P], F32, tag="mx" if i % 2 else "tp", bufs=3 if i % 2 else 4)
            if i in (1, 2):
                keep_warm(xt[:].rearrange("p s r -> p (s r)"))
            for s in range(PASSES_1 * 2):
                nc.tensor.transpose(xt[:, s, :], x_words[:, s * P : (s + 1) * P], ident_f32[:])
            x_banks[i] = xt

        def copy_x(i):
            if i in x_grouped:
                return
            x_grouped_tile = work.tile(
                [P, PASSES_1, P, PACK], BF16, align_bytes=64, tag="x_grouped", bufs=TILES
            )
            x_grouped[i] = x_grouped_tile
            nc.scalar.copy(
                out=x_grouped[i][:].bitcast(F32),
                in_=x_banks[i][:].rearrange("p (g u) r -> p g r u", u=2),
            )

        def quant_x(i):
            if i in x_mx:
                return
            codes = work.tile([P, PASSES_1, P], U32, align_bytes=64, tag="x_codes", bufs=TILES)
            scales = work.tile([P, PASSES_1, P], U8, align_bytes=64, tag="x_scales", bufs=TILES)
            quantise(
                nc,
                x_grouped[i][:].rearrange("p g r t -> p (g r t)"),
                codes[:].rearrange("p g r -> p (g r)"),
                scales[:].rearrange("p g r -> p (g r)"),
            )
            x_mx[i] = (codes, scales)

        def mx1(i):
            codes, scales = x_mx[i]
            z1_tile = psum.tile([P, D], F32, tag="mx", bufs=3)
            z1[i] = z1_tile
            for g in range(PASSES_1):
                nc.tensor.matmul_mx(
                    out=z1[i][:],
                    lhsT=codes[:, g, :].bitcast(FP8X4),
                    lhsT_scale=scales[:, g, :],
                    rhs=w1_codes[:, g, :].bitcast(FP8X4),
                    rhs_scale=w1_scales[:, g, :],
                    start=(g == 0),
                    stop=(g == PASSES_1 - 1),
                )

        def bias1(i):
            pre1_tile = work.tile([P, D], F32, tag="pre1", bufs=TILES)
            pre1[i] = pre1_tile
            nc.vector.tensor_tensor(out=pre1[i][:], in0=z1[i][:], in1=b1_full[:], op=ALU.add)

        def relu1(i):
            a1_tile = work.tile([P, D], F32, tag="a1", bufs=TILES)
            tok[i] = a1_tile
            nc.scalar.activation(out=tok[i][:], in_=pre1[i][:], func=ACT.Relu, accum_out=total1[:, i : i + 1])

        def mean1(i):
            if i % 2:
                nc.scalar.mul(out=neg_mean1[:, i - 1 : i + 1], in_=total1[:, i - 1 : i + 1], mul=-1.0 / D)

        def centre1(i):
            cen1_tile = work.tile([P, D], F32, tag="cen1", bufs=TILES)
            cen1[i] = cen1_tile
            nc.vector.scalar_tensor_tensor(
                out=cen1[i][:],
                in0=tok[i][:],
                scalar=neg_mean1[:, i : i + 1],
                in1=g1_full[:],
                op0=ALU.add,
                op1=ALU.mult,
            )

        def square1(i):
            squares = work.tile([P, D], F32, tag="squares", bufs=2)
            nc.scalar.activation(
                out=squares[:], in_=tok[i][:], func=ACT.Square,
                bias=neg_mean1[:, i : i + 1], accum_out=sq_dev1[:, i : i + 1],
            )

        def inv1(i):
            if i % 2:
                nc.scalar.activation(
                    out=rstd1[:, i - 1 : i + 1], in_=sq_dev1[:, i - 1 : i + 1],
                    func=ACT.Abs_reciprocal_sqrt, bias=eps_col[:], scale=1.0 / D,
                )

        def scale1(i):
            u1_tile = work.tile([P, D], F32, tag="u1", bufs=TILES)
            u1[i] = u1_tile
            nc.vector.scalar_tensor_tensor(
                out=u1[i][:], in0=cen1[i][:], scalar=rstd1[:, i : i + 1], in1=s1_b2_bank[:],
                op0=ALU.mult, op1=ALU.add,
            )

        def trans_h(i):
            ht_tile = psum.tile([P, PACK, P], F32, tag="tp", bufs=4)
            ht[i] = ht_tile
            nc.tensor.matmul(
                out=ht[i][:].rearrange("p t r -> p (t r)"), lhsT=shift_rows[:],
                rhs=minus_blocks[:].rearrange("k t r -> k (t r)"), start=True, stop=False,
            )
            for t in range(PACK):
                nc.tensor.matmul(
                    out=ht[i][:, t, :], lhsT=u1[i][:, block(t)], rhs=ident_f32[:],
                    is_transpose=True, start=False, stop=(t == PACK - 1),
                )

        def round_h(i):
            h_grouped_tile = work.tile([P, P, PACK], BF16, align_bytes=64, tag="h_grouped", bufs=TILES)
            h_grouped[i] = h_grouped_tile
            nc.scalar.copy(out=h_grouped[i][:], in_=ht[i][:].rearrange("p t r -> p r t"))

        def quant_h(i):
            codes = work.tile([P, P], U32, align_bytes=64, tag="h_codes", bufs=TILES)
            scales = work.tile([P, P], U8, align_bytes=64, tag="h_scales", bufs=TILES)
            quantise(nc, h_grouped[i][:].rearrange("p r t -> p (r t)"), codes[:], scales[:])
            h_mx[i] = (codes, scales)

        def second(i):
            codes, scales = h_mx[i]
            z2_tile = psum.tile([P, D], F32, tag="mx", bufs=3)
            z2[i] = z2_tile
            nc.tensor.matmul_mx(
                out=z2[i][:],
                lhsT=codes[:].bitcast(FP8X4),
                lhsT_scale=scales[:],
                rhs=w2_codes[:].bitcast(FP8X4),
                rhs_scale=w2_scales[:],
                start=True,
                stop=True,
            )

        def residual(i):
            act2_tile = work.tile([P, D], F32, tag="pre2", bufs=TILES)
            act2[i] = act2_tile
            nc.vector.tensor_tensor(out=act2[i][:], in0=z2[i][:], in1=u1[i][:], op=ALU.add)

        def relu2(i):
            act = work.tile([P, D], F32, tag="act2", bufs=TILES)
            if i in SUM_ON_VECTOR:
                nc.vector.tensor_scalar(
                    out=act[:], in0=act2[i][:], scalar1=0.0, scalar2=None, op0=ALU.max, op1=ALU.add,
                    accum_out=total2[:, i : i + 1],
                )
            else:
                nc.scalar.activation(out=act[:], in_=act2[i][:], func=ACT.Relu, accum_out=total2[:, i : i + 1])
            act2[i] = act

        def stat_cols(i):
            if i >= TILES - 2:
                return slice(i, i + 1)
            return slice(i - 1, i + 1) if i % 2 else None

        def mean2(i):
            cols = stat_cols(i)
            if cols:
                nc.scalar.mul(out=neg_mean2[:, cols], in_=total2[:, cols], mul=-1.0 / D)

        def centre2(i):
            cen2_tile = work.tile([P, D], F32, tag="cen2", bufs=TILES)
            cen2[i] = cen2_tile
            cols = slice(0, POOL_FROM.get(i, D))
            if cols.stop:
                nc.vector.scalar_tensor_tensor(
                    out=cen2[i][:, cols], in0=act2[i][:, cols], scalar=neg_mean2[:, i : i + 1],
                    in1=affine2[0][:, 0, cols], op0=ALU.add, op1=ALU.mult,
                )

        def square2(i):
            squares = work.tile([P, D], F32, tag="squares", bufs=2)
            nc.scalar.activation(
                out=squares[:], in_=act2[i][:], func=ACT.Square,
                bias=neg_mean2[:, i : i + 1], accum_out=sq_dev2[:, i : i + 1],
            )

        def inv2(i):
            cols = stat_cols(i)
            if cols:
                nc.scalar.activation(
                    out=rstd2[:, cols], in_=sq_dev2[:, cols],
                    func=ACT.Abs_reciprocal_sqrt, bias=eps_col[:], scale=1.0 / D,
                )

        pool_results = {}

        def store_pool(i):
            if i in POOL_FROM:
                nc.sync.dma_start(out=pool_results[i][0], in_=pool_results[i][1])

        def scale2(i):
            result = work.tile([P, D], F32, tag="result", bufs=TILES)
            j, e = i // 2, i % 2
            pair = out[2 * j * P : (2 * j + 2) * P, :].rearrange("(p e) c -> p e c", e=2)
            width = POOL_FROM.get(i, D)
            if width < D:
                cols = slice(width, D)
                gained = work.tile([P, D], F32, tag="gained2", bufs=3)
                nc.gpsimd.tensor_scalar(
                    out=cen2[i][:, cols], in0=act2[i][:, cols], scalar1=neg_mean2[:, i : i + 1],
                    scalar2=rstd2[:, i : i + 1], op0=ALU.add, op1=ALU.mult,
                )
                nc.gpsimd.tensor_tensor(out=gained[:, cols], in0=cen2[i][:, cols], in1=g2_full[:, cols], op=ALU.mult)
                nc.gpsimd.tensor_tensor(out=result[:, cols], in0=gained[:, cols], in1=s2_full[:, cols], op=ALU.add)
                pool_results[i] = (pair[:, e, cols], result[:, cols])
            if width == 0:
                return
            pieces = 2 if i == TILES - 1 else 1
            for n in range(pieces):
                cols = slice(n * width // pieces, (n + 1) * width // pieces)
                nc.vector.scalar_tensor_tensor(
                    out=result[:, cols], in0=cen2[i][:, cols], scalar=rstd2[:, i : i + 1], in1=affine2[0][:, 1, cols],
                    op0=ALU.mult, op1=ALU.add,
                )
                nc.sync.dma_start(out=pair[:, e, cols], in_=result[:, cols])

        b1_bank = psum.tile([P, D], F32, tag="mx", bufs=3)
        nc.tensor.matmul(
            out=b1_bank[:], lhsT=ident_bf16[:, 0:1].to_broadcast([P, P]), rhs=b1_row[:], start=True, stop=True
        )
        b1_full = const.tile([P, D], F32)
        nc.scalar.copy(out=b1_full[:], in_=b1_bank[:])
        idle_bank = psum.tile([P, D], F32, tag="tp", bufs=4)
        for n in range(2):
            nc.tensor.matmul(out=idle_bank[:, block(n)], lhsT=ident_f32[:], rhs=ident_f32[:], start=True, stop=True)
        w1_grouped = {}

        for g in range(PASSES_1):
            w_grouped = work.tile([P, D, PACK], BF16, align_bytes=64, tag="w_grouped", bufs=3)
            w1_grouped[g] = w_grouped

        def w1_regroup(g, cols=slice(0, D)):
            regroup(nc.vector.tensor_copy, w1_grouped[g][:, cols, :], w1_raw[:, g, :, cols])

        def w1_quant(g, cols=slice(0, D)):
            quantise(
                nc, w1_grouped[g][:, cols, :].rearrange("p c t -> p (c t)"), w1_codes[:, g, cols], w1_scales[:, g, cols]
            )

        halves = (slice(0, D // 2), slice(D // 2, D))
        for cols in halves:
            w1_regroup(0, cols)
        for cols in halves:
            w1_quant(0, cols)
        w1_regroup(1)
        trans_x(0)
        copy_x(0)
        quant_x(0)
        w1_quant(1)

        s1_b2_bank = psum.tile([P, D], F32, tag="affine", bufs=1)
        affine2 = {}
        affine_cols = const.tile([P, 2 * BLOCKS], BF16)
        w2_grouped = work.tile([P, D, PACK], BF16, align_bytes=64, tag="w_grouped", bufs=3)

        shift_cols = const.tile([P, 2 * BLOCKS], F32)
        sum_cols = const.tile([P, BLOCKS], F32)

        def sum_shift(i):
            if i == 0:
                turned = psum.tile([P, P], BF16, tag="tp", bufs=4)
                nc.tensor.transpose(turned[:], shift_rows[:], ident_bf16[:])
                nc.scalar.copy(out=shift_cols[:], in_=turned[:, 0 : 2 * BLOCKS])
                nc.scalar.copy(out=affine_cols[:], in_=turned[:, 2 * BLOCKS : 4 * BLOCKS])
                nc.gpsimd.tensor_tensor(
                    out=sum_cols[:], in0=shift_cols[:, 0:BLOCKS], in1=shift_cols[:, BLOCKS : 2 * BLOCKS], op=ALU.add
                )
            if i == 1:
                for t in range(BLOCKS):
                    nc.tensor.transpose(
                        s1_b2_bank[:, block(t)], sum_cols[:, t : t + 1].to_broadcast([P, P]), ident_f32[:]
                    )

        def spread2(i):
            if i == TILES - 1:
                bank = psum.tile([P, 2, D], BF16, tag="affine", bufs=1)
                affine2[0] = bank
                for t in range(2 * BLOCKS):
                    nc.tensor.transpose(
                        bank[:, t // BLOCKS, block(t % BLOCKS)],
                        affine_cols[:, t : t + 1].to_broadcast([P, P]), ident_bf16[:],
                    )

        def w2_regroup(i):
            if i < 4:
                cols = slice(i * D // 4, (i + 1) * D // 4)
                nc.scalar.copy(
                    out=w2_grouped[:, cols, :].rearrange("p (c i) t -> p c t i", i=4),
                    in_=w2_raw[:, :, cols].rearrange("p t (c i) -> p c t i", i=4),
                )

        def w2_quant(i):
            if i == 0:
                quantise(nc, w2_grouped[:].rearrange("p c t -> p (c t)"), w2_codes[:], w2_scales[:])

        stages = [
            (20, second),
            (20, spread2),
            (33, store_pool),
            (0, trans_x),
            (3, mx1),
            (14, trans_h),
            (22, residual),
            (12, scale1),
            (3, bias1),
            (17, quant_h),
            (1, quant_x),
            (17, w2_quant),
            (6, mean1),
            (5, relu1),
            (24, mean2),
            (23, relu2),
            (15, round_h),
            (0, copy_x),
            (12, w2_regroup),
            (8, centre1),
            (27, centre2),
            (29, scale2),
            (10, sum_shift),
            (9, inv1),
            (7, square1),
            (26, inv2),
            (25, square2),
        ]
        for step in range(TILES + max(lag for lag, stage in stages)):
            for lag, stage in stages:
                if 0 <= step - lag < TILES:
                    stage(step - lag)
